import numpy as np
import ml_dtypes


def mxq(x, axis, fmt="e4m3"):
    dtype, down = {"e4m3": (ml_dtypes.float8_e4m3fn, 7), "e5m2": (ml_dtypes.float8_e5m2, 14)}[fmt]
    v = np.moveaxis(np.asarray(x, np.float32).astype(ml_dtypes.bfloat16).astype(np.float64), axis, -1)
    blocks = v.reshape(v.shape[:-1] + (-1, 32))
    amax = np.abs(blocks).max(-1, keepdims=True)
    byte = np.maximum(np.where(amax > 0, np.frexp(amax)[1] - 1 + 127, 0) - down, 1)
    scale = np.exp2(byte - 127.0)
    codes = (blocks / scale).astype(np.float32).astype(dtype).astype(np.float64)
    return np.moveaxis((codes * scale).reshape(v.shape), -1, axis)


WIDE = False


def mx_kscale(k):
    if not WIDE:
        return np.ones(k)
    levels = np.array([10, -10, 5, -5, 0])
    if k % 512:
        return np.exp2(np.random.permutation(np.resize(levels, k // 32))).repeat(32)
    a = np.empty((k // 512, 16))
    for p in range(k // 512):
        a[p, :8] = np.random.permutation(np.resize(levels, 8))
        for g in range(8):
            far = levels[np.abs(levels - a[p, g]) >= 10]
            a[p, g + 8] = far[np.random.randint(len(far))]
    return np.exp2(a.ravel()).repeat(32)


BF16 = ml_dtypes.bfloat16


def bf(x):
    return np.asarray(x, np.float32).astype(BF16)


def f64(x):
    return np.asarray(x).astype(np.float64)


B, H, W, C, F, K, G, RR = 4, 32, 32, 1024, 256, 3, 16, 4
KK = K * K
P = B * H * W


def setup_inputs():
    s = mx_kscale(C)
    return {"x": bf(np.random.standard_normal((B, H, W, C)) * s),
            "Wi": bf(np.random.standard_normal((C, F)) / np.sqrt(C) / s[:, None]),
            "bi": bf(np.random.standard_normal(F) * 0.3),
            "w_span": bf(np.random.standard_normal((B, H, W, KK * G)) * 0.7)}


def reference(x, Wi, bi, w_span):
    xi = ((mxq(f64(x).reshape(P, C), 1, "e4m3") @ mxq(f64(Wi), 0, "e4m3")) + f64(bi)).reshape(B, H, W, F)
    pad = (K - 1) // 2
    xp = np.pad(xi, ((0, 0), (pad, pad), (pad, pad), (0, 0)))
    patches = np.stack([xp[:, i:i + H, j:j + W, :] for i in range(K) for j in range(K)], axis=-2)
    patches = patches.reshape(B, H, W, G, F // G, KK)
    w = f64(w_span).reshape(B, H, W, G, KK)[:, :, :, :, None, :]
    return (w * patches).sum(-1).reshape(B, H, W, F)

@@ -1,0 +1,291 @@
+from contextlib import ExitStack
+
+import concourse.mybir as mybir
+from concourse.masks import make_identity
+
+F32 = mybir.dt.float32
+BF16 = mybir.dt.bfloat16
+U32 = mybir.dt.uint32
+U8 = mybir.dt.uint8
+FP8X4 = mybir.dt.float8_e4m3fn_x4
+MULT = mybir.AluOpType.mult
+ADD = mybir.AluOpType.add
+
+P = 128
+
+IMAGES, HEIGHT, WIDTH = 4, 32, 32
+C_IN, C_OUT = 1024, 256
+WINDOW = 3
+TAPS = WINDOW * WINDOW
+GROUPS = 16
+GROUP_CHANNELS = C_OUT // GROUPS
+GROUP_LEN = GROUP_CHANNELS * TAPS
+PIXELS = IMAGES * HEIGHT * WIDTH
+
+FLOPS = 2 * PIXELS * C_IN * C_OUT + 2 * PIXELS * TAPS * C_OUT
+
+K_PASS = 4 * P
+PASSES = C_IN // K_PASS
+WORDS_PASS = K_PASS // 2
+C_HALVES = C_OUT // P
+CHUNK = 256
+CHUNK_TILES = CHUNK // P
+CHUNK_ROWS = CHUNK // WIDTH
+CHUNKS = PIXELS // CHUNK
+CHUNKS_IMAGE = HEIGHT // CHUNK_ROWS
+PADDED_ROWS = HEIGHT + 2
+BLOCK_F32 = 8
+
+TILE_ROWS = P // WIDTH
+BANK = 512
+P_HALF = TAPS * C_OUT // 2
+HALF_GROUPS = GROUPS // 2
+HALF_OUT = C_OUT // 2
+BANK_GROUPS = BANK // GROUP_LEN
+GPSIMD_OUT = 72
+HALVES_CHUNK = 2 * CHUNK_TILES
+
+LOAD_AHEAD = 3
+QUANTISE_LAG = 1
+PROJECT_LAG = 2
+INVOLVE_LAG = 3
+
+
+def tile_involution2d_pa_kernel(tc, x, Wi, bi, w_span, out):
+    nc = tc.nc
+    x_rows = x.rearrange("b u v k -> (b u v) k")
+    w_rows = w_span.rearrange("b u v c -> (b u v) c")
+    out_rows = out.rearrange("b u v o -> (b u v) o")
+
+    with ExitStack() as ctx:
+        ctx.enter_context(tc.manual_schedule())
+        const = ctx.enter_context(tc.tile_pool(name="const", bufs=1))
+        x_pool = ctx.enter_context(tc.tile_pool(name="x", bufs=LOAD_AHEAD + 1))
+        mx_pool = ctx.enter_context(tc.tile_pool(name="mx", bufs=2))
+        q_pool = ctx.enter_context(tc.tile_pool(name="q", bufs=2))
+        sum_pool = ctx.enter_context(tc.tile_pool(name="sums", bufs=1))
+        out_pool = ctx.enter_context(tc.tile_pool(name="out", bufs=2))
+        xt_psum = ctx.enter_context(tc.psum_pool(name="xt", bufs=2))
+        xi_psum = ctx.enter_context(tc.psum_pool(name="xi", bufs=1))
+        p_psum = ctx.enter_context(tc.psum_pool(name="p", bufs=5))
+
+        x_tiles = {}
+        grouped_tiles = {}
+        code_tiles = {}
+
+        def load_x(c):
+            x_sb = x_pool.tile([P, CHUNK_TILES * C_IN], BF16, name="x_sb")
+            nc.sync.dma_start(
+                out=x_sb[:].rearrange("p (n k) -> p n k", n=CHUNK_TILES),
+                in_=x_rows[c * CHUNK : (c + 1) * CHUNK, :].rearrange("(n p) k -> p n k", p=P),
+            )
+            x_tiles[c] = x_sb
+
+        load_x(0)
+        wi_raw = const.tile([P, PASSES * 4 * C_OUT], BF16, name="wi_raw")
+        nc.sync.dma_start(
+            out=wi_raw[:].rearrange("p (g tc) -> p g tc", g=PASSES),
+            in_=Wi.rearrange("(g q t) c -> q g (t c)", q=P, t=4),
+        )
+        bias_rows = const.tile([P, P], BF16, name="bias_rows")
+        nc.vector.memset(bias_rows[:], 0.0)
+        nc.sync.dma_start(out=bias_rows[0:C_HALVES, :], in_=bi.rearrange("(h c) -> h c", h=C_HALVES))
+        for c in range(1, LOAD_AHEAD):
+            load_x(c)
+
+        shifter = const.tile([P, 2 * P], F32, name="shifter")
+        make_identity(nc, shifter[:, 0:P])
+        nc.gpsimd.memset(shifter[:, P : 2 * P], 0.0)
+        identity = shifter[:, 0:P]
+
+        wi_grouped = const.tile([P, PASSES * C_OUT * 4], BF16, name="wi_grouped", align_bytes=64)
+        nc.vector.tensor_copy(
+            out=wi_grouped[:].rearrange("p (g c t) -> p g c t", g=PASSES, t=4),
+            in_=wi_raw[:].rearrange("p (g t c) -> p g c t", g=PASSES, t=4),
+        )
+        wi_codes = const.tile([P, PASSES * C_OUT], U32, name="wi_codes", align_bytes=64)
+        wi_scales = const.tile([P, PASSES * C_OUT], U8, name="wi_scales", align_bytes=64)
+        nc.vector.quantize_mx(out=wi_codes[:].bitcast(FP8X4), scales=wi_scales[:], in_=wi_grouped[:])
+
+        bias_rows_f32 = const.tile([P, P], F32, name="bias_rows_f32")
+        nc.vector.tensor_copy(out=bias_rows_f32[:], in_=bias_rows[:])
+        bias_ps = xt_psum.tile([P, P], F32, name="bias_ps", tag="xt")
+        nc.tensor.transpose(bias_ps[:], bias_rows_f32[:], identity)
+        bias_cols = const.tile([P, C_HALVES], F32, name="bias_cols")
+        nc.vector.tensor_copy(out=bias_cols[:], in_=bias_ps[:, 0:C_HALVES])
+
+        w_sb = const.tile([P, (PIXELS // P) * GROUPS * TAPS], BF16, name="w_sb")
+        w_tiles = w_sb[:].rearrange("p (n c) -> p n c", c=GROUPS * TAPS)
+        tiles_image = HEIGHT // TILE_ROWS
+        for b in range(IMAGES):
+            nc.sync.dma_start(
+                out=w_tiles[:, b * tiles_image : (b + 1) * tiles_image, :],
+                in_=w_rows[b * HEIGHT * WIDTH : (b + 1) * HEIGHT * WIDTH, :].rearrange(
+                    "(n p) c -> p n c", p=P
+                ),
+            )
+
+        shifted = []
+        for j in range(WINDOW):
+            xi_sb = const.tile([P, C_HALVES * IMAGES * PADDED_ROWS * WIDTH], F32, name="xi_sb%d" % j)
+            view = xi_sb[:].rearrange(
+                "p (h b r v) -> p h b r v", h=C_HALVES, b=IMAGES, r=PADDED_ROWS
+            )
+            nc.gpsimd.memset(view[:, :, :, 0, :], 0.0)
+            nc.gpsimd.memset(view[:, :, :, PADDED_ROWS - 1, :], 0.0)
+            shifted.append(view)
+        nc.gpsimd.memset(shifted[0][:, :, :, :, 0:BLOCK_F32], 0.0)
+        nc.gpsimd.memset(shifted[WINDOW - 1][:, :, :, :, WIDTH - BLOCK_F32 : WIDTH], 0.0)
+
+        def transpose_x(c):
+            x_words = x_tiles[c][:].bitcast(F32)
+            grouped = mx_pool.tile([P, PASSES * CHUNK * 4], BF16, name="grouped", align_bytes=64)
+            grouped_words = grouped[:].bitcast(F32).rearrange(
+                "p (g r u) -> p g r u", g=PASSES, u=2
+            )
+            for n in range(CHUNK_TILES):
+                xt = xt_psum.tile([P, 2 * PASSES, P], F32, name="xt", tag="xt")
+                for s in range(2 * PASSES):
+                    first = n * (C_IN // 2) + (s // 2) * WORDS_PASS
+                    nc.tensor.transpose(
+                        xt[:, s, :], x_words[:, first + s % 2 : first + WORDS_PASS : 2], identity
+                    )
+                nc.scalar.copy(
+                    out=grouped_words[:, :, n * P : (n + 1) * P, :],
+                    in_=xt[:].rearrange("p (g u) r -> p g r u", u=2),
+                )
+            grouped_tiles[c] = grouped
+
+        def quantise_x(c):
+            codes = mx_pool.tile([P, PASSES * CHUNK], U32, name="codes", align_bytes=64)
+            scales = mx_pool.tile([P, PASSES * CHUNK], U8, name="scales", align_bytes=64)
+            nc.vector.quantize_mx(
+                out=codes[:].bitcast(FP8X4), scales=scales[:], in_=grouped_tiles[c][:]
+            )
+            code_tiles[c] = (codes, scales)
+
+        def project(c):
+            codes, scales = code_tiles[c]
+            xi_ps = xi_psum.tile([P, C_HALVES, CHUNK], F32, name="xi_ps")
+            for h in range(C_HALVES):
+                for g in range(PASSES):
+                    wi_cols = slice(g * C_OUT + h * P, g * C_OUT + (h + 1) * P)
+                    x_cols = slice(g * CHUNK, (g + 1) * CHUNK)
+                    nc.tensor.matmul_mx(
+                        out=xi_ps[:, h, :],
+                        lhsT=wi_codes[:, wi_cols].bitcast(FP8X4),
+                        lhsT_scale=wi_scales[:, wi_cols],
+                        rhs=codes[:, x_cols].bitcast(FP8X4),
+                        rhs_scale=scales[:, x_cols],
+                        start=(g == 0),
+                        stop=(g == PASSES - 1),
+                    )
+            b = c // CHUNKS_IMAGE
+            first_row = 1 + (c % CHUNKS_IMAGE) * CHUNK_ROWS
+            for h in range(C_HALVES):
+                xi_rows = xi_ps[:, h, :].rearrange("p (r v) -> p r v", v=WIDTH)
+                for j in range(WINDOW):
+                    lo = max(0, 1 - j)
+                    hi = min(WIDTH, WIDTH + 1 - j)
+                    nc.scalar.activation(
+                        out=shifted[j][:, h, b, first_row : first_row + CHUNK_ROWS, lo:hi],
+                        in_=xi_rows[:, :, lo + j - 1 : hi + j - 1],
+                        func=mybir.ActivationFunctionType.Identity,
+                        bias=bias_cols[:, h : h + 1],
+                        scale=1.0,
+                    )
+
+        def involve(c, to_quantise):
+            b = c // CHUNKS_IMAGE
+            q = q_pool.tile([P, HALVES_CHUNK * P_HALF], F32, name="q")
+            for n in range(CHUNK_TILES):
+                tile_index = c * CHUNK_TILES + n
+                top = (c % CHUNKS_IMAGE) * CHUNK_ROWS + n * TILE_ROWS
+                for half in range(2):
+                    for g0 in reversed(range(0, HALF_GROUPS, BANK_GROUPS)):
+                        groups = min(BANK_GROUPS, HALF_GROUPS - g0)
+                        first = half * P_HALF + g0 * GROUP_LEN
+                        last = first + groups * GROUP_LEN
+                        p_ps = p_psum.tile([P, BANK], F32, name="p_ps")
+                        for block in range(first // P, (last + P - 1) // P):
+                            t, h = block // C_HALVES, block % C_HALVES
+                            i, j = t // WINDOW, t % WINDOW
+                            column = max(0, block * P - first)
+                            shift = max(0, first - block * P)
+                            nc.tensor.transpose(
+                                p_ps[:, column : column + P],
+                                shifted[j][:, h, b, top + i : top + i + TILE_ROWS, :].rearrange(
+                                    "p r v -> p (r v)"
+                                ),
+                                shifter[:, shift : shift + P],
+                            )
+                        if (n, half, g0) == (CHUNK_TILES - 1, 1, 0) and to_quantise < CHUNKS:
+                            quantise_x(to_quantise)
+                        w_first = (half * HALF_GROUPS + g0) * TAPS
+                        at = (n * 2 + half) * P_HALF + g0 * GROUP_LEN
+                        nc.vector.tensor_tensor(
+                            out=q[:, at : at + groups * GROUP_LEN].rearrange(
+                                "p (g c m) -> p g c m", c=GROUP_CHANNELS, m=TAPS
+                            ),
+                            in0=p_ps[:, 0 : groups * GROUP_LEN].rearrange(
+                                "p (g c m) -> p g c m", c=GROUP_CHANNELS, m=TAPS
+                            ),
+                            in1=w_tiles[:, tile_index, w_first : w_first + groups * TAPS]
+                            .rearrange("p (g m) -> p g m", m=TAPS)
+                            .unsqueeze(2)
+                            .to_broadcast([P, groups, GROUP_CHANNELS, TAPS]),
+                            op=MULT,
+                        )
+
+            gpsimd_out = GPSIMD_OUT if c < CHUNKS - 1 else 0
+            terms = q[:].rearrange("p (a o m) -> p a o m", a=HALVES_CHUNK, m=TAPS)
+            result = out_pool.tile([P, HALVES_CHUNK * HALF_OUT], F32, name="result")
+            result_halves = result[:].rearrange("p (a o) -> p a o", a=HALVES_CHUNK)
+            nc.vector.tensor_reduce(
+                out=result_halves[:, :, gpsimd_out:HALF_OUT],
+                in_=terms[:, :, gpsimd_out:HALF_OUT, :],
+                axis=mybir.AxisListType.X,
+                op=ADD,
+            )
+            if gpsimd_out > 0:
+                count = HALVES_CHUNK * gpsimd_out
+                sum4 = sum_pool.tile([P, count * 4], F32, name="sum4")
+                sum2 = sum_pool.tile([P, count * 2], F32, name="sum2")
+                sum1 = sum_pool.tile([P, count], F32, name="sum1")
+                nc.gpsimd.tensor_tensor(
+                    out=sum4[:].rearrange("p (a o m) -> p a o m", a=HALVES_CHUNK, m=4),
+                    in0=terms[:, :, 0:gpsimd_out, 0:4],
+                    in1=terms[:, :, 0:gpsimd_out, 4:8],
+                    op=ADD,
+                )
+                fours = sum4[:].rearrange("p (o m) -> p o m", m=4)
+                nc.gpsimd.tensor_tensor(
+                    out=sum2[:].rearrange("p (o m) -> p o m", m=2),
+                    in0=fours[:, :, 0:2],
+                    in1=fours[:, :, 2:4],
+                    op=ADD,
+                )
+                twos = sum2[:].rearrange("p (o m) -> p o m", m=2)
+                nc.gpsimd.tensor_tensor(out=sum1[:], in0=twos[:, :, 0], in1=twos[:, :, 1], op=ADD)
+                nc.gpsimd.tensor_tensor(
+                    out=result_halves[:, :, 0:gpsimd_out],
+                    in0=sum1[:].rearrange("p (a o) -> p a o", a=HALVES_CHUNK),
+                    in1=terms[:, :, 0:gpsimd_out, 8],
+                    op=ADD,
+                )
+            nc.sync.dma_start(
+                out=out_rows[c * CHUNK : (c + 1) * CHUNK, :].rearrange("(n p) o -> p n o", p=P),
+                in_=result[:].rearrange("p (n o) -> p n o", n=CHUNK_TILES),
+            )
+
+        for step in range(CHUNKS + INVOLVE_LAG):
+            if step + LOAD_AHEAD < CHUNKS:
+                load_x(step + LOAD_AHEAD)
+            if 0 <= step - PROJECT_LAG < CHUNKS:
+                project(step - PROJECT_LAG)
+            if step >= INVOLVE_LAG:
+                involve(step - INVOLVE_LAG, step - QUANTISE_LAG)
+            elif step >= QUANTISE_LAG:
+                quantise_x(step - QUANTISE_LAG)
+            if step < CHUNKS:
+                transpose_x(step)

@@ -27,59 +27,58 @@ FLOPS = 2 * PIXELS * C_IN * C_OUT + 2 * PIXELS * TAPS * C_OUT
 K_PASS = 4 * P
 PASSES = C_IN // K_PASS
 WORDS_PASS = K_PASS // 2
-C_HALVES = C_OUT // P
-CHUNK = 256
-CHUNK_TILES = CHUNK // P
-CHUNK_ROWS = CHUNK // WIDTH
-CHUNKS = PIXELS // CHUNK
-CHUNKS_IMAGE = HEIGHT // CHUNK_ROWS
-PADDED_ROWS = HEIGHT + 2
-BLOCK_F32 = 8
+ROW_LEN = WINDOW * C_OUT
+P_LEN = TAPS * C_OUT
+HALF = C_OUT // 2
 
-TILE_ROWS = P // WIDTH
-BANK = 512
-P_HALF = TAPS * C_OUT // 2
-HALF_GROUPS = GROUPS // 2
-HALF_OUT = C_OUT // 2
-BANK_GROUPS = BANK // GROUP_LEN
-GPSIMD_OUT = 72
-HALVES_CHUNK = 2 * CHUNK_TILES
+PAIR = 2
+PAIRS = HEIGHT // PAIR
+BAND = 4
+VEC_GROUPS = 11
+VEC_W = VEC_GROUPS * TAPS
 
-LOAD_AHEAD = 3
+LOAD_AHEAD = 2
 QUANTISE_LAG = 1
-PROJECT_LAG = 2
 INVOLVE_LAG = 3
+SUM_LAG = 4
+BACK_LAG = 5
 
 
 def tile_involution2d_pa_kernel(tc, x, Wi, bi, w_span, out):
     nc = tc.nc
-    x_rows = x.rearrange("b u v k -> (b u v) k")
-    w_rows = w_span.rearrange("b u v c -> (b u v) c")
-    out_rows = out.rearrange("b u v o -> (b u v) o")
+    x_img = x.rearrange("b u v k -> b v u k")
+    w_img = w_span.rearrange("b u v c -> b v u c")
+    out_img = out.rearrange("b u v o -> b v u o")
 
     with ExitStack() as ctx:
         ctx.enter_context(tc.manual_schedule())
         const = ctx.enter_context(tc.tile_pool(name="const", bufs=1))
-        x_pool = ctx.enter_context(tc.tile_pool(name="x", bufs=LOAD_AHEAD + 1))
+        x_pool = ctx.enter_context(tc.tile_pool(name="x", bufs=3))
         mx_pool = ctx.enter_context(tc.tile_pool(name="mx", bufs=2))
-        q_pool = ctx.enter_context(tc.tile_pool(name="q", bufs=2))
-        sum_pool = ctx.enter_context(tc.tile_pool(name="sums", bufs=1))
+        q_pool = ctx.enter_context(tc.tile_pool(name="q", bufs=5))
         out_pool = ctx.enter_context(tc.tile_pool(name="out", bufs=2))
         xt_psum = ctx.enter_context(tc.psum_pool(name="xt", bufs=2))
         xi_psum = ctx.enter_context(tc.psum_pool(name="xi", bufs=1))
-        p_psum = ctx.enter_context(tc.psum_pool(name="p", bufs=5))
+        w_psum = ctx.enter_context(tc.psum_pool(name="wp", bufs=2))
+        sum_psum = ctx.enter_context(tc.psum_pool(name="sum", bufs=2))
+        back_psum = ctx.enter_context(tc.psum_pool(name="back", bufs=1))
 
         x_tiles = {}
         grouped_tiles = {}
         code_tiles = {}
+        q_tiles = {}
+        sum_tiles = {}
+        result_tiles = {}
 
-        def load_x(c):
-            x_sb = x_pool.tile([P, CHUNK_TILES * C_IN], BF16, name="x_sb")
-            nc.sync.dma_start(
-                out=x_sb[:].rearrange("p (n k) -> p n k", n=CHUNK_TILES),
-                in_=x_rows[c * CHUNK : (c + 1) * CHUNK, :].rearrange("(n p) k -> p n k", p=P),
-            )
-            x_tiles[c] = x_sb
+        def load_x(band):
+            x_sb = x_pool.tile([P, BAND * C_IN], BF16, name="x_sb")
+            view = x_sb[:].rearrange("p (r k) -> p r k", r=BAND)
+            step = PAIR if band == 0 else BAND
+            for r in range(0, BAND, step):
+                for b in range(IMAGES):
+                    u = band * BAND + r
+                    nc.sync.dma_start(out=view[b:P:IMAGES, r : r + step, :], in_=x_img[b, :, u : u + step, :])
+            x_tiles[band] = x_sb
 
         load_x(0)
         wi_raw = const.tile([P, PASSES * 4 * C_OUT], BF16, name="wi_raw")
@@ -87,16 +86,33 @@ def tile_involution2d_pa_kernel(tc, x, Wi, bi, w_span, out):
             out=wi_raw[:].rearrange("p (g tc) -> p g tc", g=PASSES),
             in_=Wi.rearrange("(g q t) c -> q g (t c)", q=P, t=4),
         )
-        bias_rows = const.tile([P, P], BF16, name="bias_rows")
+        bias_rows = const.tile([P, C_OUT], BF16, name="bias_rows")
         nc.vector.memset(bias_rows[:], 0.0)
-        nc.sync.dma_start(out=bias_rows[0:C_HALVES, :], in_=bi.rearrange("(h c) -> h c", h=C_HALVES))
-        for c in range(1, LOAD_AHEAD):
-            load_x(c)
+        nc.sync.dma_start(out=bias_rows[0:1, :], in_=bi.unsqueeze(0))
+        ones = const.tile([P, P], BF16, name="ones")
+        nc.vector.memset(ones[:], 1.0)
+        load_x(1)
+        w_sb = const.tile([P, HEIGHT * GROUPS * TAPS], BF16, name="w_sb")
+        w_rows = w_sb[:].rearrange("p (u c) -> p u c", u=HEIGHT)
+        for first in range(0, HEIGHT, HEIGHT // 2):
+            for b in range(IMAGES):
+                nc.sync.dma_start(
+                    out=w_rows[b:P:IMAGES, first : first + HEIGHT // 2, :],
+                    in_=w_img[b, :, first : first + HEIGHT // 2, :],
+                )
 
-        shifter = const.tile([P, 2 * P], F32, name="shifter")
-        make_identity(nc, shifter[:, 0:P])
-        nc.gpsimd.memset(shifter[:, P : 2 * P], 0.0)
-        identity = shifter[:, 0:P]
+        identity = const.tile([P, P], F32, name="identity")
+        make_identity(nc, identity[:])
+        identity_bf = const.tile([P, P], BF16, name="identity_bf")
+        make_identity(nc, identity_bf[:])
+
+        window = const.tile([P, (HEIGHT + 2) * ROW_LEN], F32, name="window")
+        window_rows = window[:].rearrange("p (r j c) -> p r j c", j=WINDOW, c=C_OUT)
+        nc.gpsimd.memset(window_rows[:, 0, :, :], 0.0)
+        for r in range(1, HEIGHT + 1, BAND * 2):
+            nc.gpsimd.memset(window_rows[0:IMAGES, r : r + BAND * 2, 0, :], 0.0)
+            nc.gpsimd.memset(window_rows[96:P, r : r + BAND * 2, 2, :], 0.0)
+        nc.gpsimd.memset(window_rows[:, HEIGHT + 1, :, :], 0.0)
 
         wi_grouped = const.tile([P, PASSES * C_OUT * 4], BF16, name="wi_grouped", align_bytes=64)
         nc.vector.tensor_copy(
@@ -107,185 +123,159 @@ def tile_involution2d_pa_kernel(tc, x, Wi, bi, w_span, out):
         wi_scales = const.tile([P, PASSES * C_OUT], U8, name="wi_scales", align_bytes=64)
         nc.vector.quantize_mx(out=wi_codes[:].bitcast(FP8X4), scales=wi_scales[:], in_=wi_grouped[:])
 
-        bias_rows_f32 = const.tile([P, P], F32, name="bias_rows_f32")
-        nc.vector.tensor_copy(out=bias_rows_f32[:], in_=bias_rows[:])
-        bias_ps = xt_psum.tile([P, P], F32, name="bias_ps", tag="xt")
-        nc.tensor.transpose(bias_ps[:], bias_rows_f32[:], identity)
-        bias_cols = const.tile([P, C_HALVES], F32, name="bias_cols")
-        nc.vector.tensor_copy(out=bias_cols[:], in_=bias_ps[:, 0:C_HALVES])
+        bias_ps = xi_psum.tile([P, PAIR, C_OUT], F32, name="bias_ps", tag="xi")
+        nc.tensor.matmul(bias_ps[:, 0, :], lhsT=ones[:], rhs=bias_rows[:], start=True, stop=True)
+        bias = const.tile([P, C_OUT], F32, name="bias")
+        nc.scalar.copy(out=bias[:], in_=bias_ps[:, 0, :])
 
-        w_sb = const.tile([P, (PIXELS // P) * GROUPS * TAPS], BF16, name="w_sb")
-        w_tiles = w_sb[:].rearrange("p (n c) -> p n c", c=GROUPS * TAPS)
-        tiles_image = HEIGHT // TILE_ROWS
-        for b in range(IMAGES):
-            nc.sync.dma_start(
-                out=w_tiles[:, b * tiles_image : (b + 1) * tiles_image, :],
-                in_=w_rows[b * HEIGHT * WIDTH : (b + 1) * HEIGHT * WIDTH, :].rearrange(
-                    "(n p) c -> p n c", p=P
-                ),
-            )
-
-        shifted = []
-        for j in range(WINDOW):
-            xi_sb = const.tile([P, C_HALVES * IMAGES * PADDED_ROWS * WIDTH], F32, name="xi_sb%d" % j)
-            view = xi_sb[:].rearrange(
-                "p (h b r v) -> p h b r v", h=C_HALVES, b=IMAGES, r=PADDED_ROWS
-            )
-            nc.gpsimd.memset(view[:, :, :, 0, :], 0.0)
-            nc.gpsimd.memset(view[:, :, :, PADDED_ROWS - 1, :], 0.0)
-            shifted.append(view)
-        nc.gpsimd.memset(shifted[0][:, :, :, :, 0:BLOCK_F32], 0.0)
-        nc.gpsimd.memset(shifted[WINDOW - 1][:, :, :, :, WIDTH - BLOCK_F32 : WIDTH], 0.0)
-
-        def transpose_x(c):
-            x_words = x_tiles[c][:].bitcast(F32)
-            grouped = mx_pool.tile([P, PASSES * CHUNK * 4], BF16, name="grouped", align_bytes=64)
-            grouped_words = grouped[:].bitcast(F32).rearrange(
-                "p (g r u) -> p g r u", g=PASSES, u=2
-            )
-            for n in range(CHUNK_TILES):
-                xt = xt_psum.tile([P, 2 * PASSES, P], F32, name="xt", tag="xt")
+        def transpose_x(k):
+            words = x_tiles[k * PAIR // BAND][:].bitcast(F32)
+            grouped = mx_pool.tile([P, PAIR * PASSES * P * 4], BF16, name="grouped", align_bytes=64)
+            grouped_words = grouped[:].bitcast(F32).rearrange("p (n g r u) -> p n g r u", n=PAIR, g=PASSES, u=2)
+            for n in range(PAIR):
+                xt = xt_psum.tile([P, 2 * PASSES, P], F32, name="xt")
                 for s in range(2 * PASSES):
-                    first = n * (C_IN // 2) + (s // 2) * WORDS_PASS
-                    nc.tensor.transpose(
-                        xt[:, s, :], x_words[:, first + s % 2 : first + WORDS_PASS : 2], identity
-                    )
-                nc.scalar.copy(
-                    out=grouped_words[:, :, n * P : (n + 1) * P, :],
-                    in_=xt[:].rearrange("p (g u) r -> p g r u", u=2),
-                )
-            grouped_tiles[c] = grouped
+                    first = ((k * PAIR) % BAND + n) * (C_IN // 2) + (s // 2) * WORDS_PASS
+                    nc.tensor.transpose(xt[:, s, :], words[:, first + s % 2 : first + WORDS_PASS : 2], identity[:])
+                nc.scalar.copy(out=grouped_words[:, n], in_=xt[:].rearrange("p (g u) r -> p g r u", u=2))
+            grouped_tiles[k] = grouped
 
-        def quantise_x(c):
-            codes = mx_pool.tile([P, PASSES * CHUNK], U32, name="codes", align_bytes=64)
-            scales = mx_pool.tile([P, PASSES * CHUNK], U8, name="scales", align_bytes=64)
-            nc.vector.quantize_mx(
-                out=codes[:].bitcast(FP8X4), scales=scales[:], in_=grouped_tiles[c][:]
-            )
-            code_tiles[c] = (codes, scales)
+        def quantise_x(k):
+            codes = mx_pool.tile([P, PAIR * PASSES * P], U32, name="codes", align_bytes=64)
+            scales = mx_pool.tile([P, PAIR * PASSES * P], U8, name="scales", align_bytes=64)
+            nc.vector.quantize_mx(out=codes[:].bitcast(FP8X4), scales=scales[:], in_=grouped_tiles[k][:])
+            code_tiles[k] = (codes, scales)
 
-        def project(c):
-            codes, scales = code_tiles[c]
-            xi_ps = xi_psum.tile([P, C_HALVES, CHUNK], F32, name="xi_ps")
-            for h in range(C_HALVES):
+        xi_tiles = {}
+
+        def project(k):
+            codes, scales = code_tiles[k]
+            xi_ps = xi_psum.tile([P, PAIR, C_OUT], F32, name="xi_ps", tag="xi")
+            for n in range(PAIR):
                 for g in range(PASSES):
-                    wi_cols = slice(g * C_OUT + h * P, g * C_OUT + (h + 1) * P)
-                    x_cols = slice(g * CHUNK, (g + 1) * CHUNK)
+                    x_cols = slice((n * PASSES + g) * P, (n * PASSES + g + 1) * P)
+                    wi_cols = slice(g * C_OUT, (g + 1) * C_OUT)
                     nc.tensor.matmul_mx(
-                        out=xi_ps[:, h, :],
-                        lhsT=wi_codes[:, wi_cols].bitcast(FP8X4),
-                        lhsT_scale=wi_scales[:, wi_cols],
-                        rhs=codes[:, x_cols].bitcast(FP8X4),
-                        rhs_scale=scales[:, x_cols],
+                        out=xi_ps[:, n, :],
+                        lhsT=codes[:, x_cols].bitcast(FP8X4),
+                        lhsT_scale=scales[:, x_cols],
+                        rhs=wi_codes[:, wi_cols].bitcast(FP8X4),
+                        rhs_scale=wi_scales[:, wi_cols],
                         start=(g == 0),
                         stop=(g == PASSES - 1),
                     )
-            b = c // CHUNKS_IMAGE
-            first_row = 1 + (c % CHUNKS_IMAGE) * CHUNK_ROWS
-            for h in range(C_HALVES):
-                xi_rows = xi_ps[:, h, :].rearrange("p (r v) -> p r v", v=WIDTH)
-                for j in range(WINDOW):
-                    lo = max(0, 1 - j)
-                    hi = min(WIDTH, WIDTH + 1 - j)
-                    nc.scalar.activation(
-                        out=shifted[j][:, h, b, first_row : first_row + CHUNK_ROWS, lo:hi],
-                        in_=xi_rows[:, :, lo + j - 1 : hi + j - 1],
-                        func=mybir.ActivationFunctionType.Identity,
-                        bias=bias_cols[:, h : h + 1],
-                        scale=1.0,
-                    )
+            xi_tiles[k] = xi_ps
 
-        def involve(c, to_quantise):
-            b = c // CHUNKS_IMAGE
-            q = q_pool.tile([P, HALVES_CHUNK * P_HALF], F32, name="q")
-            for n in range(CHUNK_TILES):
-                tile_index = c * CHUNK_TILES + n
-                top = (c % CHUNKS_IMAGE) * CHUNK_ROWS + n * TILE_ROWS
-                for half in range(2):
-                    for g0 in reversed(range(0, HALF_GROUPS, BANK_GROUPS)):
-                        groups = min(BANK_GROUPS, HALF_GROUPS - g0)
-                        first = half * P_HALF + g0 * GROUP_LEN
-                        last = first + groups * GROUP_LEN
-                        p_ps = p_psum.tile([P, BANK], F32, name="p_ps")
-                        for block in range(first // P, (last + P - 1) // P):
-                            t, h = block // C_HALVES, block % C_HALVES
-                            i, j = t // WINDOW, t % WINDOW
-                            column = max(0, block * P - first)
-                            shift = max(0, first - block * P)
-                            nc.tensor.transpose(
-                                p_ps[:, column : column + P],
-                                shifted[j][:, h, b, top + i : top + i + TILE_ROWS, :].rearrange(
-                                    "p r v -> p (r v)"
-                                ),
-                                shifter[:, shift : shift + P],
-                            )
-                        if (n, half, g0) == (CHUNK_TILES - 1, 1, 0) and to_quantise < CHUNKS:
-                            quantise_x(to_quantise)
-                        w_first = (half * HALF_GROUPS + g0) * TAPS
-                        at = (n * 2 + half) * P_HALF + g0 * GROUP_LEN
-                        nc.vector.tensor_tensor(
-                            out=q[:, at : at + groups * GROUP_LEN].rearrange(
-                                "p (g c m) -> p g c m", c=GROUP_CHANNELS, m=TAPS
-                            ),
-                            in0=p_ps[:, 0 : groups * GROUP_LEN].rearrange(
-                                "p (g c m) -> p g c m", c=GROUP_CHANNELS, m=TAPS
-                            ),
-                            in1=w_tiles[:, tile_index, w_first : w_first + groups * TAPS]
-                            .rearrange("p (g m) -> p g m", m=TAPS)
-                            .unsqueeze(2)
-                            .to_broadcast([P, groups, GROUP_CHANNELS, TAPS]),
-                            op=MULT,
-                        )
-
-            gpsimd_out = GPSIMD_OUT if c < CHUNKS - 1 else 0
-            terms = q[:].rearrange("p (a o m) -> p a o m", a=HALVES_CHUNK, m=TAPS)
-            result = out_pool.tile([P, HALVES_CHUNK * HALF_OUT], F32, name="result")
-            result_halves = result[:].rearrange("p (a o) -> p a o", a=HALVES_CHUNK)
-            nc.vector.tensor_reduce(
-                out=result_halves[:, :, gpsimd_out:HALF_OUT],
-                in_=terms[:, :, gpsimd_out:HALF_OUT, :],
-                axis=mybir.AxisListType.X,
+        def add_bias(k):
+            r = 1 + k * PAIR
+            nc.vector.tensor_tensor(
+                out=window_rows[:, r : r + PAIR, 1, :],
+                in0=xi_tiles[k][:],
+                in1=bias[:].unsqueeze(1).to_broadcast([P, PAIR, C_OUT]),
                 op=ADD,
             )
-            if gpsimd_out > 0:
-                count = HALVES_CHUNK * gpsimd_out
-                sum4 = sum_pool.tile([P, count * 4], F32, name="sum4")
-                sum2 = sum_pool.tile([P, count * 2], F32, name="sum2")
-                sum1 = sum_pool.tile([P, count], F32, name="sum1")
-                nc.gpsimd.tensor_tensor(
-                    out=sum4[:].rearrange("p (a o m) -> p a o m", a=HALVES_CHUNK, m=4),
-                    in0=terms[:, :, 0:gpsimd_out, 0:4],
-                    in1=terms[:, :, 0:gpsimd_out, 4:8],
-                    op=ADD,
-                )
-                fours = sum4[:].rearrange("p (o m) -> p o m", m=4)
-                nc.gpsimd.tensor_tensor(
-                    out=sum2[:].rearrange("p (o m) -> p o m", m=2),
-                    in0=fours[:, :, 0:2],
-                    in1=fours[:, :, 2:4],
-                    op=ADD,
-                )
-                twos = sum2[:].rearrange("p (o m) -> p o m", m=2)
-                nc.gpsimd.tensor_tensor(out=sum1[:], in0=twos[:, :, 0], in1=twos[:, :, 1], op=ADD)
-                nc.gpsimd.tensor_tensor(
-                    out=result_halves[:, :, 0:gpsimd_out],
-                    in0=sum1[:].rearrange("p (a o) -> p a o", a=HALVES_CHUNK),
-                    in1=terms[:, :, 0:gpsimd_out, 8],
-                    op=ADD,
-                )
-            nc.sync.dma_start(
-                out=out_rows[c * CHUNK : (c + 1) * CHUNK, :].rearrange("(n p) o -> p n o", p=P),
-                in_=result[:].rearrange("p (n o) -> p n o", n=CHUNK_TILES),
-            )
 
-        for step in range(CHUNKS + INVOLVE_LAG):
-            if step + LOAD_AHEAD < CHUNKS:
-                load_x(step + LOAD_AHEAD)
-            if 0 <= step - PROJECT_LAG < CHUNKS:
-                project(step - PROJECT_LAG)
-            if step >= INVOLVE_LAG:
-                involve(step - INVOLVE_LAG, step - QUANTISE_LAG)
-            elif step >= QUANTISE_LAG:
-                quantise_x(step - QUANTISE_LAG)
-            if step < CHUNKS:
+        def shift(k):
+            r = 1 + k * PAIR
+            rows = slice(r, r + PAIR)
+            for lo, hi in ((0, 64), (64, P - IMAGES)):
+                nc.sync.dma_start(
+                    out=window_rows[lo + IMAGES : hi + IMAGES, rows, 0, :], in_=window_rows[lo:hi, rows, 1, :]
+                )
+                nc.sync.dma_start(
+                    out=window_rows[lo:hi, rows, 2, :], in_=window_rows[lo + IMAGES : hi + IMAGES, rows, 1, :]
+                )
+
+        w_gate = {}
+        w_ps_tiles = {}
+
+        def weights(j):
+            w_ps = w_psum.tile([P, PAIR, VEC_W], F32, name="w_ps")
+            nc.tensor.matmul(
+                w_ps[:], lhsT=identity_bf[:], rhs=w_rows[:, j * PAIR : (j + 1) * PAIR, 0:VEC_W], start=True, stop=True
+            )
+            w_ps_tiles[j] = w_ps
+
+        def gate(j):
+            wg = mx_pool.tile([P, PAIR, GROUPS * TAPS - VEC_W], BF16, name="wg")
+            nc.vector.tensor_copy(out=wg[:], in_=w_rows[:, j * PAIR : (j + 1) * PAIR, VEC_W:])
+            w_gate[j] = wg
+
+        def product(j, n):
+            q = q_pool.tile([P, P_LEN], F32, name="q")
+            u = j * PAIR + n
+            split = VEC_GROUPS * GROUP_LEN
+            for engine, lo, hi, w in (
+                (nc.vector, 0, split, w_ps_tiles[j][:, n, :]),
+                (nc.gpsimd, split, P_LEN, w_gate[j][:, n, :]),
+            ):
+                groups = (hi - lo) // GROUP_LEN
+                engine.tensor_tensor(
+                    out=q[:, lo:hi].rearrange("p (g c m) -> p g c m", c=GROUP_CHANNELS, m=TAPS),
+                    in0=window[:, u * ROW_LEN + lo : u * ROW_LEN + hi].rearrange(
+                        "p (g c m) -> p g c m", c=GROUP_CHANNELS, m=TAPS
+                    ),
+                    in1=w.rearrange("p (g m) -> p g m", m=TAPS)
+                    .unsqueeze(2)
+                    .to_broadcast([P, groups, GROUP_CHANNELS, TAPS]),
+                    op=MULT,
+                )
+            q_tiles[j, n] = q
+
+        def sums(j):
+            sum_ps = sum_psum.tile([P, PAIR * 2, P], F32, name="sum_ps")
+            for n in range(PAIR):
+                terms = q_tiles[j, n][:].rearrange("p (o m) -> p o m", m=TAPS)
+                for half in range(2):
+                    for m in range(TAPS):
+                        nc.tensor.matmul(
+                            sum_ps[:, n * 2 + half, :],
+                            lhsT=terms[:, half * HALF : (half + 1) * HALF, m],
+                            rhs=identity[:],
+                            start=(m == 0),
+                            stop=(m == TAPS - 1),
+                            is_transpose=True,
+                        )
+            sum_sb = mx_pool.tile([P, PAIR * 2, P], F32, name="sum_sb")
+            nc.scalar.copy(out=sum_sb[:], in_=sum_ps[:])
+            sum_tiles[j] = sum_sb
+
+        def back(j):
+            back_ps = back_psum.tile([P, PAIR * 2, P], F32, name="back_ps")
+            for a in range(PAIR * 2):
+                nc.tensor.transpose(back_ps[:, a, :], sum_tiles[j][:, a, :], identity[:])
+            if j * PAIR % BAND == 0:
+                result_tiles[j * PAIR // BAND] = out_pool.tile([P, BAND, C_OUT], F32, name="result")
+            result = result_tiles[j * PAIR // BAND]
+            r = j * PAIR % BAND
+            nc.scalar.copy(
+                out=result[:, r : r + PAIR, :].rearrange("p r (h o) -> p (r h) o", h=2), in_=back_ps[:]
+            )
+            if r + PAIR == BAND:
+                u = j * PAIR + PAIR - BAND
+                for b in range(IMAGES):
+                    nc.sync.dma_start(out=out_img[b, :, u : u + BAND, :], in_=result[b:P:IMAGES, :, :])
+
+        for step in range(PAIRS + BACK_LAG):
+            if step * PAIR % BAND == 0 and step * PAIR // BAND + LOAD_AHEAD < HEIGHT // BAND:
+                load_x(step * PAIR // BAND + LOAD_AHEAD)
+            if step < PAIRS:
                 transpose_x(step)
+            j = step - INVOLVE_LAG
+            k = step - QUANTISE_LAG
+            if 0 <= k < PAIRS:
+                quantise_x(k)
+            if 0 <= j < PAIRS:
+                gate(j)
+                weights(j)
+                product(j, 0)
+            if 0 <= k < PAIRS:
+                project(k)
+                add_bias(k)
+                shift(k)
+            if 0 <= j < PAIRS:
+                product(j, 1)
+            if 0 <= step - SUM_LAG < PAIRS:
+                sums(step - SUM_LAG)
+            if 0 <= step - BACK_LAG < PAIRS:
+                back(step - BACK_LAG)

@@ -34,7 +34,7 @@ HALF = C_OUT // 2
 PAIR = 2
 PAIRS = HEIGHT // PAIR
 BAND = 4
-VEC_GROUPS = 11
+VEC_GROUPS = 8
 VEC_W = VEC_GROUPS * TAPS
 
 LOAD_AHEAD = 2
@@ -55,8 +55,8 @@ def tile_involution2d_pa_kernel(tc, x, Wi, bi, w_span, out):
         const = ctx.enter_context(tc.tile_pool(name="const", bufs=1))
         x_pool = ctx.enter_context(tc.tile_pool(name="x", bufs=3))
         mx_pool = ctx.enter_context(tc.tile_pool(name="mx", bufs=2))
-        q_pool = ctx.enter_context(tc.tile_pool(name="q", bufs=5))
-        out_pool = ctx.enter_context(tc.tile_pool(name="out", bufs=2))
+        q_pool = ctx.enter_context(tc.tile_pool(name="q", bufs=6))
+        out_pool = ctx.enter_context(tc.tile_pool(name="out", bufs=3))
         xt_psum = ctx.enter_context(tc.psum_pool(name="xt", bufs=2))
         xi_psum = ctx.enter_context(tc.psum_pool(name="xi", bufs=1))
         w_psum = ctx.enter_context(tc.psum_pool(name="wp", bufs=2))
@@ -222,35 +222,44 @@ def tile_involution2d_pa_kernel(tc, x, Wi, bi, w_span, out):
                 )
             q_tiles[j, n] = q
 
+        def result_of(j):
+            band = j * PAIR // BAND
+            if band not in result_tiles:
+                result_tiles[band] = out_pool.tile([P, BAND, C_OUT], F32, name="result")
+            return result_tiles[band], j * PAIR % BAND
+
+        def vector_sum(j, n):
+            result, r = result_of(j)
+            nc.vector.tensor_reduce(
+                out=result[:, r + n, HALF:],
+                in_=q_tiles[j, n][:, HALF * TAPS :].rearrange("p (o m) -> p o m", m=TAPS),
+                axis=mybir.AxisListType.X,
+                op=ADD,
+            )
+
         def sums(j):
-            sum_ps = sum_psum.tile([P, PAIR * 2, P], F32, name="sum_ps")
+            sum_ps = sum_psum.tile([P, PAIR, P], F32, name="sum_ps")
             for n in range(PAIR):
                 terms = q_tiles[j, n][:].rearrange("p (o m) -> p o m", m=TAPS)
-                for half in range(2):
-                    for m in range(TAPS):
-                        nc.tensor.matmul(
-                            sum_ps[:, n * 2 + half, :],
-                            lhsT=terms[:, half * HALF : (half + 1) * HALF, m],
-                            rhs=identity[:],
-                            start=(m == 0),
-                            stop=(m == TAPS - 1),
-                            is_transpose=True,
-                        )
-            sum_sb = mx_pool.tile([P, PAIR * 2, P], F32, name="sum_sb")
+                for m in range(TAPS):
+                    nc.tensor.matmul(
+                        sum_ps[:, n, :],
+                        lhsT=terms[:, 0:HALF, m],
+                        rhs=identity[:],
+                        start=(m == 0),
+                        stop=(m == TAPS - 1),
+                        is_transpose=True,
+                    )
+            sum_sb = mx_pool.tile([P, PAIR, P], F32, name="sum_sb")
             nc.scalar.copy(out=sum_sb[:], in_=sum_ps[:])
             sum_tiles[j] = sum_sb
 
         def back(j):
-            back_ps = back_psum.tile([P, PAIR * 2, P], F32, name="back_ps")
-            for a in range(PAIR * 2):
-                nc.tensor.transpose(back_ps[:, a, :], sum_tiles[j][:, a, :], identity[:])
-            if j * PAIR % BAND == 0:
-                result_tiles[j * PAIR // BAND] = out_pool.tile([P, BAND, C_OUT], F32, name="result")
-            result = result_tiles[j * PAIR // BAND]
-            r = j * PAIR % BAND
-            nc.scalar.copy(
-                out=result[:, r : r + PAIR, :].rearrange("p r (h o) -> p (r h) o", h=2), in_=back_ps[:]
-            )
+            back_ps = back_psum.tile([P, PAIR, P], F32, name="back_ps")
+            for n in range(PAIR):
+                nc.tensor.transpose(back_ps[:, n, :], sum_tiles[j][:, n, :], identity[:])
+            result, r = result_of(j)
+            nc.scalar.copy(out=result[:, r : r + PAIR, 0:HALF], in_=back_ps[:])
             if r + PAIR == BAND:
                 u = j * PAIR + PAIR - BAND
                 for b in range(IMAGES):
@@ -269,6 +278,8 @@ def tile_involution2d_pa_kernel(tc, x, Wi, bi, w_span, out):
                 gate(j)
                 weights(j)
                 product(j, 0)
+            if 0 <= step - SUM_LAG < PAIRS:
+                vector_sum(step - SUM_LAG, 0)
             if 0 <= k < PAIRS:
                 project(k)
                 add_bias(k)
@@ -276,6 +287,7 @@ def tile_involution2d_pa_kernel(tc, x, Wi, bi, w_span, out):
             if 0 <= j < PAIRS:
                 product(j, 1)
             if 0 <= step - SUM_LAG < PAIRS:
+                vector_sum(step - SUM_LAG, 1)
                 sums(step - SUM_LAG)
             if 0 <= step - BACK_LAG < PAIRS:
                 back(step - BACK_LAG)

@@ -34,14 +34,16 @@ HALF = C_OUT // 2
 PAIR = 2
 PAIRS = HEIGHT // PAIR
 BAND = 4
-VEC_GROUPS = 8
-VEC_W = VEC_GROUPS * TAPS
-
-LOAD_AHEAD = 2
-QUANTISE_LAG = 1
-INVOLVE_LAG = 3
-SUM_LAG = 4
-BACK_LAG = 5
+SCALAR_FIRST = 12
+VEC_GROUPS = (8, 4)
+VEC_W = max(VEC_GROUPS) * TAPS
+NATURAL = SCALAR_FIRST * GROUP_LEN
+NATURAL_OUT = SCALAR_FIRST * GROUP_CHANNELS
+NATURAL_W = SCALAR_FIRST * TAPS
+SCALAR_OUT = C_OUT - NATURAL_OUT
+W_ROWS = 8
+LOADED = 4
+LEAD = 3
 
 
 def tile_involution2d_pa_kernel(tc, x, Wi, bi, w_span, out):
@@ -53,9 +55,9 @@ def tile_involution2d_pa_kernel(tc, x, Wi, bi, w_span, out):
     with ExitStack() as ctx:
         ctx.enter_context(tc.manual_schedule())
         const = ctx.enter_context(tc.tile_pool(name="const", bufs=1))
-        x_pool = ctx.enter_context(tc.tile_pool(name="x", bufs=3))
+        x_pool = ctx.enter_context(tc.tile_pool(name="x", bufs=4))
         mx_pool = ctx.enter_context(tc.tile_pool(name="mx", bufs=2))
-        q_pool = ctx.enter_context(tc.tile_pool(name="q", bufs=6))
+        q_pool = ctx.enter_context(tc.tile_pool(name="q", bufs=3))
         out_pool = ctx.enter_context(tc.tile_pool(name="out", bufs=3))
         xt_psum = ctx.enter_context(tc.psum_pool(name="xt", bufs=2))
         xi_psum = ctx.enter_context(tc.psum_pool(name="xi", bufs=1))
@@ -66,76 +68,76 @@ def tile_involution2d_pa_kernel(tc, x, Wi, bi, w_span, out):
         x_tiles = {}
         grouped_tiles = {}
         code_tiles = {}
+        xi_tiles = {}
         q_tiles = {}
         sum_tiles = {}
         result_tiles = {}
+        w_gate = {}
+        w_scalar = {}
+        qs_tiles = {}
+        sum_ps_tiles = {}
+        w_ps_tiles = {}
 
-        def load_x(band):
-            x_sb = x_pool.tile([P, BAND * C_IN], BF16, name="x_sb")
-            view = x_sb[:].rearrange("p (r k) -> p r k", r=BAND)
-            step = PAIR if band == 0 else BAND
-            for r in range(0, BAND, step):
-                for b in range(IMAGES):
-                    u = band * BAND + r
-                    nc.sync.dma_start(out=view[b:P:IMAGES, r : r + step, :], in_=x_img[b, :, u : u + step, :])
-            x_tiles[band] = x_sb
+        def load_x(u, rows):
+            x_sb = x_pool.tile([P, PAIR * C_IN], BF16, name="x_sb")
+            view = x_sb[:].rearrange("p (r k) -> p r k", r=PAIR)
+            for b in range(IMAGES):
+                nc.sync.dma_start(out=view[b:P:IMAGES, 0:rows, :], in_=x_img[b, :, u : u + rows, :])
+            for r in range(rows):
+                x_tiles[u + r] = (x_sb, r)
 
-        load_x(0)
+        w_tiles = {}
+
+        def load_w(u):
+            w_sb = const.tile([P, W_ROWS, GROUPS * TAPS], BF16, name="w_sb%d" % u)
+            for b in range(IMAGES):
+                nc.sync.dma_start(out=w_sb[b:P:IMAGES, :, :], in_=w_img[b, :, u : u + W_ROWS, :])
+            w_tiles[u // W_ROWS] = w_sb
+
+        load_x(0, PAIR)
         wi_raw = const.tile([P, PASSES * 4 * C_OUT], BF16, name="wi_raw")
         nc.sync.dma_start(
             out=wi_raw[:].rearrange("p (g tc) -> p g tc", g=PASSES),
             in_=Wi.rearrange("(g q t) c -> q g (t c)", q=P, t=4),
         )
+        load_x(PAIR, PAIR)
         bias_rows = const.tile([P, C_OUT], BF16, name="bias_rows")
         nc.vector.memset(bias_rows[:], 0.0)
-        nc.sync.dma_start(out=bias_rows[0:1, :], in_=bi.unsqueeze(0))
         ones = const.tile([P, P], BF16, name="ones")
         nc.vector.memset(ones[:], 1.0)
-        load_x(1)
-        w_sb = const.tile([P, HEIGHT * GROUPS * TAPS], BF16, name="w_sb")
-        w_rows = w_sb[:].rearrange("p (u c) -> p u c", u=HEIGHT)
-        for first in range(0, HEIGHT, HEIGHT // 2):
-            for b in range(IMAGES):
-                nc.sync.dma_start(
-                    out=w_rows[b:P:IMAGES, first : first + HEIGHT // 2, :],
-                    in_=w_img[b, :, first : first + HEIGHT // 2, :],
-                )
+        zeros = const.tile([P, C_OUT], F32, name="zeros")
+        nc.vector.memset(zeros[:], 0.0)
+        warm = const.tile([P, 1], F32, name="warm")
+        nc.scalar.copy(out=warm[:], in_=zeros[:, 0:1])
 
         identity = const.tile([P, P], F32, name="identity")
         make_identity(nc, identity[:])
+        nc.gpsimd.dma_start(out=bias_rows[0:1, :], in_=bi.unsqueeze(0))
         identity_bf = const.tile([P, P], BF16, name="identity_bf")
         make_identity(nc, identity_bf[:])
 
         window = const.tile([P, (HEIGHT + 2) * ROW_LEN], F32, name="window")
         window_rows = window[:].rearrange("p (r j c) -> p r j c", j=WINDOW, c=C_OUT)
         nc.gpsimd.memset(window_rows[:, 0, :, :], 0.0)
-        for r in range(1, HEIGHT + 1, BAND * 2):
-            nc.gpsimd.memset(window_rows[0:IMAGES, r : r + BAND * 2, 0, :], 0.0)
-            nc.gpsimd.memset(window_rows[96:P, r : r + BAND * 2, 2, :], 0.0)
+        load_x(2 * PAIR, PAIR)
+        for j, lo in ((0, 0), (WINDOW - 1, P - IMAGES)):
+            nc.sync.dma_start(
+                out=window_rows[lo : lo + IMAGES, 1 : HEIGHT + 1, j, :],
+                in_=zeros[lo : lo + IMAGES, :].unsqueeze(1).to_broadcast([IMAGES, HEIGHT, C_OUT]),
+            )
+        load_w(0)
+        load_x(3 * PAIR, PAIR)
         nc.gpsimd.memset(window_rows[:, HEIGHT + 1, :, :], 0.0)
 
-        wi_grouped = const.tile([P, PASSES * C_OUT * 4], BF16, name="wi_grouped", align_bytes=64)
-        nc.vector.tensor_copy(
-            out=wi_grouped[:].rearrange("p (g c t) -> p g c t", g=PASSES, t=4),
-            in_=wi_raw[:].rearrange("p (g t c) -> p g c t", g=PASSES, t=4),
-        )
-        wi_codes = const.tile([P, PASSES * C_OUT], U32, name="wi_codes", align_bytes=64)
-        wi_scales = const.tile([P, PASSES * C_OUT], U8, name="wi_scales", align_bytes=64)
-        nc.vector.quantize_mx(out=wi_codes[:].bitcast(FP8X4), scales=wi_scales[:], in_=wi_grouped[:])
-
-        bias_ps = xi_psum.tile([P, PAIR, C_OUT], F32, name="bias_ps", tag="xi")
-        nc.tensor.matmul(bias_ps[:, 0, :], lhsT=ones[:], rhs=bias_rows[:], start=True, stop=True)
-        bias = const.tile([P, C_OUT], F32, name="bias")
-        nc.scalar.copy(out=bias[:], in_=bias_ps[:, 0, :])
-
         def transpose_x(k):
-            words = x_tiles[k * PAIR // BAND][:].bitcast(F32)
             grouped = mx_pool.tile([P, PAIR * PASSES * P * 4], BF16, name="grouped", align_bytes=64)
             grouped_words = grouped[:].bitcast(F32).rearrange("p (n g r u) -> p n g r u", n=PAIR, g=PASSES, u=2)
             for n in range(PAIR):
+                x_sb, row = x_tiles[k * PAIR + n]
+                words = x_sb[:].bitcast(F32)
                 xt = xt_psum.tile([P, 2 * PASSES, P], F32, name="xt")
                 for s in range(2 * PASSES):
-                    first = ((k * PAIR) % BAND + n) * (C_IN // 2) + (s // 2) * WORDS_PASS
+                    first = row * (C_IN // 2) + (s // 2) * WORDS_PASS
                     nc.tensor.transpose(xt[:, s, :], words[:, first + s % 2 : first + WORDS_PASS : 2], identity[:])
                 nc.scalar.copy(out=grouped_words[:, n], in_=xt[:].rearrange("p (g u) r -> p g r u", u=2))
             grouped_tiles[k] = grouped
@@ -145,8 +147,6 @@ def tile_involution2d_pa_kernel(tc, x, Wi, bi, w_span, out):
             scales = mx_pool.tile([P, PAIR * PASSES * P], U8, name="scales", align_bytes=64)
             nc.vector.quantize_mx(out=codes[:].bitcast(FP8X4), scales=scales[:], in_=grouped_tiles[k][:])
             code_tiles[k] = (codes, scales)
-
-        xi_tiles = {}
 
         def project(k):
             codes, scales = code_tiles[k]
@@ -186,41 +186,60 @@ def tile_involution2d_pa_kernel(tc, x, Wi, bi, w_span, out):
                     out=window_rows[lo:hi, rows, 2, :], in_=window_rows[lo + IMAGES : hi + IMAGES, rows, 1, :]
                 )
 
-        w_gate = {}
-        w_ps_tiles = {}
+        def pair_weights(j):
+            return w_tiles[j * PAIR // W_ROWS][:, j * PAIR % W_ROWS : j * PAIR % W_ROWS + PAIR, :]
 
         def weights(j):
             w_ps = w_psum.tile([P, PAIR, VEC_W], F32, name="w_ps")
-            nc.tensor.matmul(
-                w_ps[:], lhsT=identity_bf[:], rhs=w_rows[:, j * PAIR : (j + 1) * PAIR, 0:VEC_W], start=True, stop=True
-            )
+            nc.tensor.matmul(w_ps[:], lhsT=identity_bf[:], rhs=pair_weights(j)[:, :, 0:VEC_W], start=True, stop=True)
             w_ps_tiles[j] = w_ps
 
         def gate(j):
-            wg = mx_pool.tile([P, PAIR, GROUPS * TAPS - VEC_W], BF16, name="wg")
-            nc.vector.tensor_copy(out=wg[:], in_=w_rows[:, j * PAIR : (j + 1) * PAIR, VEC_W:])
+            wg = mx_pool.tile([P, PAIR, NATURAL_W], BF16, name="wg")
+            nc.vector.tensor_copy(out=wg[:], in_=pair_weights(j)[:, :, 0:NATURAL_W])
             w_gate[j] = wg
 
-        def product(j, n):
-            q = q_pool.tile([P, P_LEN], F32, name="q")
+        def scalar_weights(j):
+            ws = mx_pool.tile([P, PAIR, GROUPS * TAPS - NATURAL_W], F32, name="ws")
+            nc.scalar.copy(out=ws[:], in_=pair_weights(j)[:, :, NATURAL_W:])
+            w_scalar[j] = ws
+
+        def new_products(j):
+            q_tiles[j] = q_pool.tile([P, PAIR, NATURAL], F32, name="q")
+            qs_tiles[j] = q_pool.tile([P, TAPS, PAIR, SCALAR_OUT], F32, name="qs")
+
+        def product(engine, j, n):
             u = j * PAIR + n
-            split = VEC_GROUPS * GROUP_LEN
-            for engine, lo, hi, w in (
-                (nc.vector, 0, split, w_ps_tiles[j][:, n, :]),
-                (nc.gpsimd, split, P_LEN, w_gate[j][:, n, :]),
-            ):
-                groups = (hi - lo) // GROUP_LEN
-                engine.tensor_tensor(
-                    out=q[:, lo:hi].rearrange("p (g c m) -> p g c m", c=GROUP_CHANNELS, m=TAPS),
-                    in0=window[:, u * ROW_LEN + lo : u * ROW_LEN + hi].rearrange(
-                        "p (g c m) -> p g c m", c=GROUP_CHANNELS, m=TAPS
-                    ),
-                    in1=w.rearrange("p (g m) -> p g m", m=TAPS)
-                    .unsqueeze(2)
-                    .to_broadcast([P, groups, GROUP_CHANNELS, TAPS]),
-                    op=MULT,
-                )
-            q_tiles[j, n] = q
+            if engine is nc.vector:
+                first, last, w = 0, VEC_GROUPS[n], w_ps_tiles[j]
+            else:
+                first, last, w = VEC_GROUPS[n], SCALAR_FIRST, w_gate[j]
+            run = slice(first * GROUP_LEN, last * GROUP_LEN)
+            engine.tensor_tensor(
+                out=q_tiles[j][:, n, run].rearrange("p (g c m) -> p g c m", c=GROUP_CHANNELS, m=TAPS),
+                in0=window[:, u * ROW_LEN + run.start : u * ROW_LEN + run.stop].rearrange(
+                    "p (g c m) -> p g c m", c=GROUP_CHANNELS, m=TAPS
+                ),
+                in1=w[:, n, first * TAPS : last * TAPS]
+                .rearrange("p (g m) -> p g m", m=TAPS)
+                .unsqueeze(2)
+                .to_broadcast([P, last - first, GROUP_CHANNELS, TAPS]),
+                op=MULT,
+            )
+
+        def scalar_product(j, n):
+            u = j * PAIR + n
+            for g in range(SCALAR_FIRST, GROUPS):
+                for m in range(TAPS):
+                    first = u * ROW_LEN + g * GROUP_LEN + m
+                    o = (g - SCALAR_FIRST) * GROUP_CHANNELS
+                    w = (g - SCALAR_FIRST) * TAPS + m
+                    nc.scalar.activation(
+                        out=qs_tiles[j][:, m, n, o : o + GROUP_CHANNELS],
+                        in_=window[:, first : first + (GROUP_CHANNELS - 1) * TAPS + 1 : TAPS],
+                        func=mybir.ActivationFunctionType.Copy,
+                        scale=w_scalar[j][:, n, w : w + 1],
+                    )
 
         def result_of(j):
             band = j * PAIR // BAND
@@ -228,66 +247,115 @@ def tile_involution2d_pa_kernel(tc, x, Wi, bi, w_span, out):
                 result_tiles[band] = out_pool.tile([P, BAND, C_OUT], F32, name="result")
             return result_tiles[band], j * PAIR % BAND
 
-        def vector_sum(j, n):
+        def vector_sum(j):
             result, r = result_of(j)
-            nc.vector.tensor_reduce(
-                out=result[:, r + n, HALF:],
-                in_=q_tiles[j, n][:, HALF * TAPS :].rearrange("p (o m) -> p o m", m=TAPS),
-                axis=mybir.AxisListType.X,
-                op=ADD,
-            )
+            for n, first in ((0, HALF), (1, 0)):
+                nc.vector.tensor_reduce(
+                    out=result[:, r + n, first:NATURAL_OUT],
+                    in_=q_tiles[j][:, n, first * TAPS :].rearrange("p (o m) -> p o m", m=TAPS),
+                    axis=mybir.AxisListType.X,
+                    op=ADD,
+                )
 
-        def sums(j):
-            sum_ps = sum_psum.tile([P, PAIR, P], F32, name="sum_ps")
-            for n in range(PAIR):
-                terms = q_tiles[j, n][:].rearrange("p (o m) -> p o m", m=TAPS)
-                for m in range(TAPS):
-                    nc.tensor.matmul(
-                        sum_ps[:, n, :],
-                        lhsT=terms[:, 0:HALF, m],
-                        rhs=identity[:],
-                        start=(m == 0),
-                        stop=(m == TAPS - 1),
-                        is_transpose=True,
-                    )
-            sum_sb = mx_pool.tile([P, PAIR, P], F32, name="sum_sb")
-            nc.scalar.copy(out=sum_sb[:], in_=sum_ps[:])
+        def tensor_sum(j, a):
+            if a == 0:
+                sum_ps_tiles[j] = sum_psum.tile([P, 2, P], F32, name="sum_ps")
+            for m in range(TAPS):
+                if a == 0:
+                    terms = q_tiles[j][:, 0, 0 : HALF * TAPS].rearrange("p (o m) -> p o m", m=TAPS)[:, :, m]
+                else:
+                    terms = qs_tiles[j][:, m, :, :].rearrange("p n o -> p (n o)")
+                nc.tensor.matmul(
+                    sum_ps_tiles[j][:, a, :],
+                    lhsT=terms,
+                    rhs=identity[:],
+                    start=(m == 0),
+                    stop=(m == TAPS - 1),
+                    is_transpose=True,
+                )
+
+        def copy_sums(j):
+            sum_sb = mx_pool.tile([P, 2, P], F32, name="sum_sb")
+            nc.scalar.copy(out=sum_sb[:], in_=sum_ps_tiles[j][:])
             sum_tiles[j] = sum_sb
 
         def back(j):
-            back_ps = back_psum.tile([P, PAIR, P], F32, name="back_ps")
-            for n in range(PAIR):
-                nc.tensor.transpose(back_ps[:, n, :], sum_tiles[j][:, n, :], identity[:])
+            back_ps = back_psum.tile([P, 2, P], F32, name="back_ps")
+            for a in range(2):
+                nc.tensor.transpose(back_ps[:, a, :], sum_tiles[j][:, a, :], identity[:])
             result, r = result_of(j)
-            nc.scalar.copy(out=result[:, r : r + PAIR, 0:HALF], in_=back_ps[:])
-            if r + PAIR == BAND:
-                u = j * PAIR + PAIR - BAND
-                for b in range(IMAGES):
-                    nc.sync.dma_start(out=out_img[b, :, u : u + BAND, :], in_=result[b:P:IMAGES, :, :])
+            nc.scalar.copy(out=result[:, r, 0:HALF], in_=back_ps[:, 0, :])
+            nc.scalar.copy(
+                out=result[:, r : r + PAIR, NATURAL_OUT:],
+                in_=back_ps[:, 1, :].rearrange("p (n o) -> p n o", n=PAIR),
+            )
 
-        for step in range(PAIRS + BACK_LAG):
-            if step * PAIR % BAND == 0 and step * PAIR // BAND + LOAD_AHEAD < HEIGHT // BAND:
-                load_x(step * PAIR // BAND + LOAD_AHEAD)
-            if step < PAIRS:
-                transpose_x(step)
-            j = step - INVOLVE_LAG
-            k = step - QUANTISE_LAG
-            if 0 <= k < PAIRS:
-                quantise_x(k)
+        def store(j):
+            rows = PAIR if j >= PAIRS - BAND // PAIR else BAND
+            u = (j + 1) * PAIR
+            if u % rows == 0:
+                result, r = result_of(j)
+                for b in range(IMAGES):
+                    nc.sync.dma_start(
+                        out=out_img[b, :, u - rows : u, :],
+                        in_=result[b:P:IMAGES, r + PAIR - rows : r + PAIR, :],
+                    )
+
+        transpose_x(0)
+        transpose_x(1)
+        wi_grouped = const.tile([P, PASSES * C_OUT * 4], BF16, name="wi_grouped", align_bytes=64)
+        nc.vector.tensor_copy(
+            out=wi_grouped[:].rearrange("p (g c t) -> p g c t", g=PASSES, t=4),
+            in_=wi_raw[:].rearrange("p (g t c) -> p g c t", g=PASSES, t=4),
+        )
+        wi_codes = const.tile([P, PASSES * C_OUT], U32, name="wi_codes", align_bytes=64)
+        wi_scales = const.tile([P, PASSES * C_OUT], U8, name="wi_scales", align_bytes=64)
+        nc.vector.quantize_mx(out=wi_codes[:].bitcast(FP8X4), scales=wi_scales[:], in_=wi_grouped[:])
+        bias_ps = back_psum.tile([P, C_OUT], F32, name="bias_ps", tag="back_ps")
+        nc.tensor.matmul(bias_ps[:], lhsT=ones[:], rhs=bias_rows[:], start=True, stop=True)
+        bias = const.tile([P, C_OUT], F32, name="bias")
+        nc.scalar.copy(out=bias[:], in_=bias_ps[:])
+
+        for j in range(-LEAD, PAIRS + 3):
+            k = j + LEAD
+            if 0 <= j - 3 < PAIRS:
+                back(j - 3)
+                store(j - 3)
+            if 0 <= j - 1 < PAIRS:
+                tensor_sum(j - 1, 0)
             if 0 <= j < PAIRS:
-                gate(j)
-                weights(j)
-                product(j, 0)
-            if 0 <= step - SUM_LAG < PAIRS:
-                vector_sum(step - SUM_LAG, 0)
-            if 0 <= k < PAIRS:
+                new_products(j)
+                scalar_product(j, 0)
+                for n in range(PAIR):
+                    product(nc.gpsimd, j, n)
+                    product(nc.vector, j, n)
+            if k < PAIRS:
+                quantise_x(k)
+            if 0 <= j + 1 < PAIRS:
+                gate(j + 1)
+                if j < 0:
+                    weights(j + 1)
+            if 0 <= j - 1 < PAIRS:
+                vector_sum(j - 1)
+            if 0 <= j - 2 < PAIRS:
+                copy_sums(j - 2)
+            if k + 1 < PAIRS and j >= 0:
+                transpose_x(k + 1)
+            if k < PAIRS:
                 project(k)
                 add_bias(k)
                 shift(k)
+            if k + 2 < PAIRS and j < -1:
+                transpose_x(k + 2)
+            if k + LOADED < PAIRS:
+                load_x((k + LOADED) * PAIR, PAIR)
+            if k % 4 == 2 and k // 4 + 1 < HEIGHT // W_ROWS:
+                load_w((k // 4 + 1) * W_ROWS)
+            if 0 <= j - 1 < PAIRS:
+                tensor_sum(j - 1, 1)
+            if 0 <= j + 1 < PAIRS:
+                if j >= 0:
+                    weights(j + 1)
+                scalar_weights(j + 1)
             if 0 <= j < PAIRS:
-                product(j, 1)
-            if 0 <= step - SUM_LAG < PAIRS:
-                vector_sum(step - SUM_LAG, 1)
-                sums(step - SUM_LAG)
-            if 0 <= step - BACK_LAG < PAIRS:
-                back(step - BACK_LAG)
+                scalar_product(j, 1)

@@ -34,14 +34,15 @@ HALF = C_OUT // 2
 PAIR = 2
 PAIRS = HEIGHT // PAIR
 BAND = 4
-SCALAR_FIRST = 12
-VEC_GROUPS = (8, 4)
+VEC_GROUPS = (8, 5)
+SCALAR_FIRST = (13, 13)
 VEC_W = max(VEC_GROUPS) * TAPS
-NATURAL = SCALAR_FIRST * GROUP_LEN
-NATURAL_OUT = SCALAR_FIRST * GROUP_CHANNELS
-NATURAL_W = SCALAR_FIRST * TAPS
-SCALAR_OUT = C_OUT - NATURAL_OUT
+NATURAL_GROUPS = max(SCALAR_FIRST)
+NATURAL = NATURAL_GROUPS * GROUP_LEN
+SCALAR_OUT = HALF // 2
+SCALAR_BASE = GROUPS - SCALAR_OUT // GROUP_CHANNELS
 W_ROWS = 8
+EXTRA_STEP = 4
 LOADED = 4
 LEAD = 3
 
@@ -129,6 +130,15 @@ def tile_involution2d_pa_kernel(tc, x, Wi, bi, w_span, out):
         load_x(3 * PAIR, PAIR)
         nc.gpsimd.memset(window_rows[:, HEIGHT + 1, :, :], 0.0)
 
+        scalar_tiles = []
+        for i in range(3):
+            qs = const.tile([P, TAPS, PAIR, SCALAR_OUT], F32, name="qs%d" % i)
+            for n in range(PAIR):
+                unused = (SCALAR_FIRST[n] - SCALAR_BASE) * GROUP_CHANNELS
+                if unused > 0:
+                    nc.gpsimd.memset(qs[:, :, n, 0:unused], 0.0)
+            scalar_tiles.append(qs)
+
         def transpose_x(k):
             grouped = mx_pool.tile([P, PAIR * PASSES * P * 4], BF16, name="grouped", align_bytes=64)
             grouped_words = grouped[:].bitcast(F32).rearrange("p (n g r u) -> p n g r u", n=PAIR, g=PASSES, u=2)
@@ -195,25 +205,25 @@ def tile_involution2d_pa_kernel(tc, x, Wi, bi, w_span, out):
             w_ps_tiles[j] = w_ps
 
         def gate(j):
-            wg = mx_pool.tile([P, PAIR, NATURAL_W], BF16, name="wg")
-            nc.vector.tensor_copy(out=wg[:], in_=pair_weights(j)[:, :, 0:NATURAL_W])
+            wg = mx_pool.tile([P, PAIR, NATURAL_GROUPS * TAPS], BF16, name="wg")
+            nc.vector.tensor_copy(out=wg[:], in_=pair_weights(j)[:, :, 0 : NATURAL_GROUPS * TAPS])
             w_gate[j] = wg
 
         def scalar_weights(j):
-            ws = mx_pool.tile([P, PAIR, GROUPS * TAPS - NATURAL_W], F32, name="ws")
-            nc.scalar.copy(out=ws[:], in_=pair_weights(j)[:, :, NATURAL_W:])
+            ws = mx_pool.tile([P, PAIR, (GROUPS - SCALAR_BASE) * TAPS], F32, name="ws")
+            nc.scalar.copy(out=ws[:], in_=pair_weights(j)[:, :, SCALAR_BASE * TAPS :])
             w_scalar[j] = ws
 
         def new_products(j):
             q_tiles[j] = q_pool.tile([P, PAIR, NATURAL], F32, name="q")
-            qs_tiles[j] = q_pool.tile([P, TAPS, PAIR, SCALAR_OUT], F32, name="qs")
+            qs_tiles[j] = scalar_tiles[j % len(scalar_tiles)]
 
         def product(engine, j, n):
             u = j * PAIR + n
             if engine is nc.vector:
                 first, last, w = 0, VEC_GROUPS[n], w_ps_tiles[j]
             else:
-                first, last, w = VEC_GROUPS[n], SCALAR_FIRST, w_gate[j]
+                first, last, w = VEC_GROUPS[n], SCALAR_FIRST[n], w_gate[j]
             run = slice(first * GROUP_LEN, last * GROUP_LEN)
             engine.tensor_tensor(
                 out=q_tiles[j][:, n, run].rearrange("p (g c m) -> p g c m", c=GROUP_CHANNELS, m=TAPS),
@@ -229,11 +239,11 @@ def tile_involution2d_pa_kernel(tc, x, Wi, bi, w_span, out):
 
         def scalar_product(j, n):
             u = j * PAIR + n
-            for g in range(SCALAR_FIRST, GROUPS):
+            for g in range(SCALAR_FIRST[n], GROUPS):
                 for m in range(TAPS):
                     first = u * ROW_LEN + g * GROUP_LEN + m
-                    o = (g - SCALAR_FIRST) * GROUP_CHANNELS
-                    w = (g - SCALAR_FIRST) * TAPS + m
+                    o = (g - SCALAR_BASE) * GROUP_CHANNELS
+                    w = (g - SCALAR_BASE) * TAPS + m
                     nc.scalar.activation(
                         out=qs_tiles[j][:, m, n, o : o + GROUP_CHANNELS],
                         in_=window[:, first : first + (GROUP_CHANNELS - 1) * TAPS + 1 : TAPS],
@@ -249,46 +259,57 @@ def tile_involution2d_pa_kernel(tc, x, Wi, bi, w_span, out):
 
         def vector_sum(j):
             result, r = result_of(j)
-            for n, first in ((0, HALF), (1, 0)):
+            for n, first in ((0, HALF), (1, HALF if j % EXTRA_STEP == 1 else 0)):
+                last = SCALAR_FIRST[n] * GROUP_CHANNELS
                 nc.vector.tensor_reduce(
-                    out=result[:, r + n, first:NATURAL_OUT],
-                    in_=q_tiles[j][:, n, first * TAPS :].rearrange("p (o m) -> p o m", m=TAPS),
+                    out=result[:, r + n, first:last],
+                    in_=q_tiles[j][:, n, first * TAPS : last * TAPS].rearrange("p (o m) -> p o m", m=TAPS),
                     axis=mybir.AxisListType.X,
                     op=ADD,
                 )
 
-        def tensor_sum(j, a):
-            if a == 0:
-                sum_ps_tiles[j] = sum_psum.tile([P, 2, P], F32, name="sum_ps")
-            for m in range(TAPS):
-                if a == 0:
-                    terms = q_tiles[j][:, 0, 0 : HALF * TAPS].rearrange("p (o m) -> p o m", m=TAPS)[:, :, m]
-                else:
-                    terms = qs_tiles[j][:, m, :, :].rearrange("p n o -> p (n o)")
-                nc.tensor.matmul(
-                    sum_ps_tiles[j][:, a, :],
-                    lhsT=terms,
-                    rhs=identity[:],
-                    start=(m == 0),
-                    stop=(m == TAPS - 1),
-                    is_transpose=True,
-                )
+        def units(j):
+            return [0, 1, None] if j % EXTRA_STEP == 1 else [0, None]
+
+        def tensor_sum(j):
+            sum_ps_tiles[j] = sum_psum.tile([P, len(units(j)), P], F32, name="sum_ps")
+            for a, n in enumerate(units(j)):
+                for m in range(TAPS):
+                    if n is None:
+                        terms = qs_tiles[j][:, m, :, :].rearrange("p n o -> p (n o)")
+                    else:
+                        terms = q_tiles[j][:, n, 0 : HALF * TAPS].rearrange("p (o m) -> p o m", m=TAPS)[:, :, m]
+                    nc.tensor.matmul(
+                        sum_ps_tiles[j][:, a, :],
+                        lhsT=terms,
+                        rhs=identity[:],
+                        start=(m == 0),
+                        stop=(m == TAPS - 1),
+                        is_transpose=True,
+                    )
 
         def copy_sums(j):
-            sum_sb = mx_pool.tile([P, 2, P], F32, name="sum_sb")
+            sum_sb = mx_pool.tile([P, len(units(j)), P], F32, name="sum_sb")
             nc.scalar.copy(out=sum_sb[:], in_=sum_ps_tiles[j][:])
             sum_tiles[j] = sum_sb
 
+        back_tiles = {}
+
         def back(j):
-            back_ps = back_psum.tile([P, 2, P], F32, name="back_ps")
-            for a in range(2):
+            back_ps = back_psum.tile([P, len(units(j)), P], F32, name="back_ps")
+            for a in range(len(units(j))):
                 nc.tensor.transpose(back_ps[:, a, :], sum_tiles[j][:, a, :], identity[:])
+            back_tiles[j] = back_ps
+
+        def copy_back(j):
+            back_ps = back_tiles[j]
             result, r = result_of(j)
-            nc.scalar.copy(out=result[:, r, 0:HALF], in_=back_ps[:, 0, :])
-            nc.scalar.copy(
-                out=result[:, r : r + PAIR, NATURAL_OUT:],
-                in_=back_ps[:, 1, :].rearrange("p (n o) -> p n o", n=PAIR),
-            )
+            rows = len(units(j)) - 1
+            nc.scalar.copy(out=result[:, r : r + rows, 0:HALF], in_=back_ps[:, 0:rows, :])
+            for n in range(PAIR):
+                first = SCALAR_FIRST[n] * GROUP_CHANNELS
+                end = (n + 1) * SCALAR_OUT
+                nc.scalar.copy(out=result[:, r + n, first:], in_=back_ps[:, rows, end - (C_OUT - first) : end])
 
         def store(j):
             rows = PAIR if j >= PAIRS - BAND // PAIR else BAND
@@ -302,7 +323,6 @@ def tile_involution2d_pa_kernel(tc, x, Wi, bi, w_span, out):
                     )
 
         transpose_x(0)
-        transpose_x(1)
         wi_grouped = const.tile([P, PASSES * C_OUT * 4], BF16, name="wi_grouped", align_bytes=64)
         nc.vector.tensor_copy(
             out=wi_grouped[:].rearrange("p (g c t) -> p g c t", g=PASSES, t=4),
@@ -315,32 +335,40 @@ def tile_involution2d_pa_kernel(tc, x, Wi, bi, w_span, out):
         nc.tensor.matmul(bias_ps[:], lhsT=ones[:], rhs=bias_rows[:], start=True, stop=True)
         bias = const.tile([P, C_OUT], F32, name="bias")
         nc.scalar.copy(out=bias[:], in_=bias_ps[:])
+        transpose_x(1)
+
+        def start_products():
+            gate(0)
+            weights(0)
+            scalar_weights(0)
+            new_products(0)
+            product(nc.gpsimd, 0, 0)
+            product(nc.vector, 0, 0)
+            scalar_product(0, 0)
 
         for j in range(-LEAD, PAIRS + 3):
             k = j + LEAD
-            if 0 <= j - 3 < PAIRS:
-                back(j - 3)
-                store(j - 3)
-            if 0 <= j - 1 < PAIRS:
-                tensor_sum(j - 1, 0)
-            if 0 <= j < PAIRS:
-                new_products(j)
-                scalar_product(j, 0)
-                for n in range(PAIR):
-                    product(nc.gpsimd, j, n)
-                    product(nc.vector, j, n)
+            new, done, moved = j - 1, j - 2, j - 3
             if k < PAIRS:
                 quantise_x(k)
-            if 0 <= j + 1 < PAIRS:
-                gate(j + 1)
-                if j < 0:
-                    weights(j + 1)
-            if 0 <= j - 1 < PAIRS:
-                vector_sum(j - 1)
-            if 0 <= j - 2 < PAIRS:
-                copy_sums(j - 2)
+            if j == -1:
+                start_products()
+            if 0 < j < PAIRS:
+                gate(j)
+                new_products(j)
+                scalar_product(j, 0)
             if k + 1 < PAIRS and j >= 0:
                 transpose_x(k + 1)
+            if 0 <= done < PAIRS:
+                copy_sums(done)
+            if 0 <= moved < PAIRS:
+                copy_back(moved)
+            if 0 <= j < PAIRS:
+                for n in range(1 if j == 0 else 0, PAIR):
+                    product(nc.gpsimd, j, n)
+                    product(nc.vector, j, n)
+            if 0 <= new < PAIRS:
+                vector_sum(new)
             if k < PAIRS:
                 project(k)
                 add_bias(k)
@@ -351,11 +379,14 @@ def tile_involution2d_pa_kernel(tc, x, Wi, bi, w_span, out):
                 load_x((k + LOADED) * PAIR, PAIR)
             if k % 4 == 2 and k // 4 + 1 < HEIGHT // W_ROWS:
                 load_w((k // 4 + 1) * W_ROWS)
-            if 0 <= j - 1 < PAIRS:
-                tensor_sum(j - 1, 1)
-            if 0 <= j + 1 < PAIRS:
-                if j >= 0:
-                    weights(j + 1)
+            if 0 <= moved < PAIRS:
+                store(moved)
+            if 0 < j + 1 < PAIRS:
+                weights(j + 1)
                 scalar_weights(j + 1)
+            if 0 <= new < PAIRS:
+                tensor_sum(new)
+            if 0 <= done < PAIRS:
+                back(done)
             if 0 <= j < PAIRS:
                 scalar_product(j, 1)

from contextlib import ExitStack

import concourse.mybir as mybir
from concourse.masks import make_identity

F32 = mybir.dt.float32
BF16 = mybir.dt.bfloat16
U32 = mybir.dt.uint32
U8 = mybir.dt.uint8
FP8X4 = mybir.dt.float8_e4m3fn_x4
MULT = mybir.AluOpType.mult
ADD = mybir.AluOpType.add

P = 128

IMAGES, HEIGHT, WIDTH = 4, 32, 32
C_IN, C_OUT = 1024, 256
WINDOW = 3
TAPS = WINDOW * WINDOW
GROUPS = 16
GROUP_CHANNELS = C_OUT // GROUPS
GROUP_LEN = GROUP_CHANNELS * TAPS
PIXELS = IMAGES * HEIGHT * WIDTH

FLOPS = 2 * PIXELS * C_IN * C_OUT + 2 * PIXELS * TAPS * C_OUT

K_PASS = 4 * P
PASSES = C_IN // K_PASS
WORDS_PASS = K_PASS // 2
ROW_LEN = WINDOW * C_OUT
P_LEN = TAPS * C_OUT
HALF = C_OUT // 2

PAIR = 2
PAIRS = HEIGHT // PAIR
BAND = 4
VEC_GROUPS = (8, 5)
SCALAR_FIRST = (13, 13)
VEC_W = max(VEC_GROUPS) * TAPS
NATURAL_GROUPS = max(SCALAR_FIRST)
NATURAL = NATURAL_GROUPS * GROUP_LEN
SCALAR_OUT = HALF // 2
SCALAR_BASE = GROUPS - SCALAR_OUT // GROUP_CHANNELS
W_ROWS = 8
EXTRA_STEP = 4
LOADED = 4
LEAD = 3


def tile_involution2d_pa_kernel(tc, x, Wi, bi, w_span, out):
    nc = tc.nc
    x_img = x.rearrange("b u v k -> b v u k")
    w_img = w_span.rearrange("b u v c -> b v u c")
    out_img = out.rearrange("b u v o -> b v u o")

    with ExitStack() as ctx:
        ctx.enter_context(tc.manual_schedule())
        const = ctx.enter_context(tc.tile_pool(name="const", bufs=1))
        x_pool = ctx.enter_context(tc.tile_pool(name="x", bufs=4))
        mx_pool = ctx.enter_context(tc.tile_pool(name="mx", bufs=2))
        q_pool = ctx.enter_context(tc.tile_pool(name="q", bufs=3))
        out_pool = ctx.enter_context(tc.tile_pool(name="out", bufs=3))
        xt_psum = ctx.enter_context(tc.psum_pool(name="xt", bufs=2))
        xi_psum = ctx.enter_context(tc.psum_pool(name="xi", bufs=1))
        w_psum = ctx.enter_context(tc.psum_pool(name="wp", bufs=2))
        sum_psum = ctx.enter_context(tc.psum_pool(name="sum", bufs=2))
        back_psum = ctx.enter_context(tc.psum_pool(name="back", bufs=1))

        x_tiles = {}
        grouped_tiles = {}
        code_tiles = {}
        xi_tiles = {}
        q_tiles = {}
        sum_tiles = {}
        result_tiles = {}
        w_gate = {}
        w_scalar = {}
        qs_tiles = {}
        sum_ps_tiles = {}
        w_ps_tiles = {}

        def load_x(u, rows):
            x_sb = x_pool.tile([P, PAIR * C_IN], BF16, name="x_sb")
            view = x_sb[:].rearrange("p (r k) -> p r k", r=PAIR)
            for b in range(IMAGES):
                nc.sync.dma_start(out=view[b:P:IMAGES, 0:rows, :], in_=x_img[b, :, u : u + rows, :])
            for r in range(rows):
                x_tiles[u + r] = (x_sb, r)

        w_tiles = {}

        def load_w(u):
            w_sb = const.tile([P, W_ROWS, GROUPS * TAPS], BF16, name="w_sb%d" % u)
            for b in range(IMAGES):
                nc.sync.dma_start(out=w_sb[b:P:IMAGES, :, :], in_=w_img[b, :, u : u + W_ROWS, :])
            w_tiles[u // W_ROWS] = w_sb

        load_x(0, PAIR)
        wi_raw = const.tile([P, PASSES * 4 * C_OUT], BF16, name="wi_raw")
        nc.sync.dma_start(
            out=wi_raw[:].rearrange("p (g tc) -> p g tc", g=PASSES),
            in_=Wi.rearrange("(g q t) c -> q g (t c)", q=P, t=4),
        )
        load_x(PAIR, PAIR)
        bias_rows = const.tile([P, C_OUT], BF16, name="bias_rows")
        nc.vector.memset(bias_rows[:], 0.0)
        ones = const.tile([P, P], BF16, name="ones")
        nc.vector.memset(ones[:], 1.0)
        zeros = const.tile([P, C_OUT], F32, name="zeros")
        nc.vector.memset(zeros[:], 0.0)
        warm = const.tile([P, 1], F32, name="warm")
        nc.scalar.copy(out=warm[:], in_=zeros[:, 0:1])

        identity = const.tile([P, P], F32, name="identity")
        make_identity(nc, identity[:])
        nc.gpsimd.dma_start(out=bias_rows[0:1, :], in_=bi.unsqueeze(0))
        identity_bf = const.tile([P, P], BF16, name="identity_bf")
        make_identity(nc, identity_bf[:])

        window = const.tile([P, (HEIGHT + 2) * ROW_LEN], F32, name="window")
        window_rows = window[:].rearrange("p (r j c) -> p r j c", j=WINDOW, c=C_OUT)
        nc.gpsimd.memset(window_rows[:, 0, :, :], 0.0)
        load_x(2 * PAIR, PAIR)
        for j, lo in ((0, 0), (WINDOW - 1, P - IMAGES)):
            nc.sync.dma_start(
                out=window_rows[lo : lo + IMAGES, 1 : HEIGHT + 1, j, :],
                in_=zeros[lo : lo + IMAGES, :].unsqueeze(1).to_broadcast([IMAGES, HEIGHT, C_OUT]),
            )
        load_w(0)
        load_x(3 * PAIR, PAIR)
        nc.gpsimd.memset(window_rows[:, HEIGHT + 1, :, :], 0.0)

        scalar_tiles = []
        for i in range(3):
            qs = const.tile([P, TAPS, PAIR, SCALAR_OUT], F32, name="qs%d" % i)
            for n in range(PAIR):
                unused = (SCALAR_FIRST[n] - SCALAR_BASE) * GROUP_CHANNELS
                if unused > 0:
                    nc.gpsimd.memset(qs[:, :, n, 0:unused], 0.0)
            scalar_tiles.append(qs)

        def transpose_x(k):
            grouped = mx_pool.tile([P, PAIR * PASSES * P * 4], BF16, name="grouped", align_bytes=64)
            grouped_words = grouped[:].bitcast(F32).rearrange("p (n g r u) -> p n g r u", n=PAIR, g=PASSES, u=2)
            for n in range(PAIR):
                x_sb, row = x_tiles[k * PAIR + n]
                words = x_sb[:].bitcast(F32)
                xt = xt_psum.tile([P, 2 * PASSES, P], F32, name="xt")
                for s in range(2 * PASSES):
                    first = row * (C_IN // 2) + (s // 2) * WORDS_PASS
                    nc.tensor.transpose(xt[:, s, :], words[:, first + s % 2 : first + WORDS_PASS : 2], identity[:])
                nc.scalar.copy(out=grouped_words[:, n], in_=xt[:].rearrange("p (g u) r -> p g r u", u=2))
            grouped_tiles[k] = grouped

        def quantise_x(k):
            codes = mx_pool.tile([P, PAIR * PASSES * P], U32, name="codes", align_bytes=64)
            scales = mx_pool.tile([P, PAIR * PASSES * P], U8, name="scales", align_bytes=64)
            nc.vector.quantize_mx(out=codes[:].bitcast(FP8X4), scales=scales[:], in_=grouped_tiles[k][:])
            code_tiles[k] = (codes, scales)

        def project(k):
            codes, scales = code_tiles[k]
            xi_ps = xi_psum.tile([P, PAIR, C_OUT], F32, name="xi_ps", tag="xi")
            for n in range(PAIR):
                for g in range(PASSES):
                    x_cols = slice((n * PASSES + g) * P, (n * PASSES + g + 1) * P)
                    wi_cols = slice(g * C_OUT, (g + 1) * C_OUT)
                    nc.tensor.matmul_mx(
                        out=xi_ps[:, n, :],
                        lhsT=codes[:, x_cols].bitcast(FP8X4),
                        lhsT_scale=scales[:, x_cols],
                        rhs=wi_codes[:, wi_cols].bitcast(FP8X4),
                        rhs_scale=wi_scales[:, wi_cols],
                        start=(g == 0),
                        stop=(g == PASSES - 1),
                    )
            xi_tiles[k] = xi_ps

        def add_bias(k):
            r = 1 + k * PAIR
            nc.vector.tensor_tensor(
                out=window_rows[:, r : r + PAIR, 1, :],
                in0=xi_tiles[k][:],
                in1=bias[:].unsqueeze(1).to_broadcast([P, PAIR, C_OUT]),
                op=ADD,
            )

        def shift(k):
            r = 1 + k * PAIR
            rows = slice(r, r + PAIR)
            for lo, hi in ((0, 64), (64, P - IMAGES)):
                nc.sync.dma_start(
                    out=window_rows[lo + IMAGES : hi + IMAGES, rows, 0, :], in_=window_rows[lo:hi, rows, 1, :]
                )
                nc.sync.dma_start(
                    out=window_rows[lo:hi, rows, 2, :], in_=window_rows[lo + IMAGES : hi + IMAGES, rows, 1, :]
                )

        def pair_weights(j):
            return w_tiles[j * PAIR // W_ROWS][:, j * PAIR % W_ROWS : j * PAIR % W_ROWS + PAIR, :]

        def weights(j):
            w_ps = w_psum.tile([P, PAIR, VEC_W], F32, name="w_ps")
            nc.tensor.matmul(w_ps[:], lhsT=identity_bf[:], rhs=pair_weights(j)[:, :, 0:VEC_W], start=True, stop=True)
            w_ps_tiles[j] = w_ps

        def gate(j):
            wg = mx_pool.tile([P, PAIR, NATURAL_GROUPS * TAPS], BF16, name="wg")
            nc.vector.tensor_copy(out=wg[:], in_=pair_weights(j)[:, :, 0 : NATURAL_GROUPS * TAPS])
            w_gate[j] = wg

        def scalar_weights(j):
            ws = mx_pool.tile([P, PAIR, (GROUPS - SCALAR_BASE) * TAPS], F32, name="ws")
            nc.scalar.copy(out=ws[:], in_=pair_weights(j)[:, :, SCALAR_BASE * TAPS :])
            w_scalar[j] = ws

        def new_products(j):
            q_tiles[j] = q_pool.tile([P, PAIR, NATURAL], F32, name="q")
            qs_tiles[j] = scalar_tiles[j % len(scalar_tiles)]

        def product(engine, j, n):
            u = j * PAIR + n
            if engine is nc.vector:
                first, last, w = 0, VEC_GROUPS[n], w_ps_tiles[j]
            else:
                first, last, w = VEC_GROUPS[n], SCALAR_FIRST[n], w_gate[j]
            run = slice(first * GROUP_LEN, last * GROUP_LEN)
            engine.tensor_tensor(
                out=q_tiles[j][:, n, run].rearrange("p (g c m) -> p g c m", c=GROUP_CHANNELS, m=TAPS),
                in0=window[:, u * ROW_LEN + run.start : u * ROW_LEN + run.stop].rearrange(
                    "p (g c m) -> p g c m", c=GROUP_CHANNELS, m=TAPS
                ),
                in1=w[:, n, first * TAPS : last * TAPS]
                .rearrange("p (g m) -> p g m", m=TAPS)
                .unsqueeze(2)
                .to_broadcast([P, last - first, GROUP_CHANNELS, TAPS]),
                op=MULT,
            )

        def scalar_product(j, n):
            u = j * PAIR + n
            for g in range(SCALAR_FIRST[n], GROUPS):
                for m in range(TAPS):
                    first = u * ROW_LEN + g * GROUP_LEN + m
                    o = (g - SCALAR_BASE) * GROUP_CHANNELS
                    w = (g - SCALAR_BASE) * TAPS + m
                    nc.scalar.activation(
                        out=qs_tiles[j][:, m, n, o : o + GROUP_CHANNELS],
                        in_=window[:, first : first + (GROUP_CHANNELS - 1) * TAPS + 1 : TAPS],
                        func=mybir.ActivationFunctionType.Copy,
                        scale=w_scalar[j][:, n, w : w + 1],
                    )

        def result_of(j):
            band = j * PAIR // BAND
            if band not in result_tiles:
                result_tiles[band] = out_pool.tile([P, BAND, C_OUT], F32, name="result")
            return result_tiles[band], j * PAIR % BAND

        def vector_sum(j):
            result, r = result_of(j)
            for n, first in ((0, HALF), (1, HALF if j % EXTRA_STEP == 1 else 0)):
                last = SCALAR_FIRST[n] * GROUP_CHANNELS
                nc.vector.tensor_reduce(
                    out=result[:, r + n, first:last],
                    in_=q_tiles[j][:, n, first * TAPS : last * TAPS].rearrange("p (o m) -> p o m", m=TAPS),
                    axis=mybir.AxisListType.X,
                    op=ADD,
                )

        def units(j):
            return [0, 1, None] if j % EXTRA_STEP == 1 else [0, None]

        def tensor_sum(j):
            sum_ps_tiles[j] = sum_psum.tile([P, len(units(j)), P], F32, name="sum_ps")
            for a, n in enumerate(units(j)):
                for m in range(TAPS):
                    if n is None:
                        terms = qs_tiles[j][:, m, :, :].rearrange("p n o -> p (n o)")
                    else:
                        terms = q_tiles[j][:, n, 0 : HALF * TAPS].rearrange("p (o m) -> p o m", m=TAPS)[:, :, m]
                    nc.tensor.matmul(
                        sum_ps_tiles[j][:, a, :],
                        lhsT=terms,
                        rhs=identity[:],
                        start=(m == 0),
                        stop=(m == TAPS - 1),
                        is_transpose=True,
                    )

        def copy_sums(j):
            sum_sb = mx_pool.tile([P, len(units(j)), P], F32, name="sum_sb")
            nc.scalar.copy(out=sum_sb[:], in_=sum_ps_tiles[j][:])
            sum_tiles[j] = sum_sb

        back_tiles = {}

        def back(j):
            back_ps = back_psum.tile([P, len(units(j)), P], F32, name="back_ps")
            for a in range(len(units(j))):
                nc.tensor.transpose(back_ps[:, a, :], sum_tiles[j][:, a, :], identity[:])
            back_tiles[j] = back_ps

        def copy_back(j):
            back_ps = back_tiles[j]
            result, r = result_of(j)
            rows = len(units(j)) - 1
            nc.scalar.copy(out=result[:, r : r + rows, 0:HALF], in_=back_ps[:, 0:rows, :])
            for n in range(PAIR):
                first = SCALAR_FIRST[n] * GROUP_CHANNELS
                end = (n + 1) * SCALAR_OUT
                nc.scalar.copy(out=result[:, r + n, first:], in_=back_ps[:, rows, end - (C_OUT - first) : end])

        def store(j):
            rows = PAIR if j >= PAIRS - BAND // PAIR else BAND
            u = (j + 1) * PAIR
            if u % rows == 0:
                result, r = result_of(j)
                for b in range(IMAGES):
                    nc.sync.dma_start(
                        out=out_img[b, :, u - rows : u, :],
                        in_=result[b:P:IMAGES, r + PAIR - rows : r + PAIR, :],
                    )

        transpose_x(0)
        wi_grouped = const.tile([P, PASSES * C_OUT * 4], BF16, name="wi_grouped", align_bytes=64)
        nc.vector.tensor_copy(
            out=wi_grouped[:].rearrange("p (g c t) -> p g c t", g=PASSES, t=4),
            in_=wi_raw[:].rearrange("p (g t c) -> p g c t", g=PASSES, t=4),
        )
        wi_codes = const.tile([P, PASSES * C_OUT], U32, name="wi_codes", align_bytes=64)
        wi_scales = const.tile([P, PASSES * C_OUT], U8, name="wi_scales", align_bytes=64)
        nc.vector.quantize_mx(out=wi_codes[:].bitcast(FP8X4), scales=wi_scales[:], in_=wi_grouped[:])
        bias_ps = back_psum.tile([P, C_OUT], F32, name="bias_ps", tag="back_ps")
        nc.tensor.matmul(bias_ps[:], lhsT=ones[:], rhs=bias_rows[:], start=True, stop=True)
        bias = const.tile([P, C_OUT], F32, name="bias")
        nc.scalar.copy(out=bias[:], in_=bias_ps[:])
        transpose_x(1)

        def start_products():
            gate(0)
            weights(0)
            scalar_weights(0)
            new_products(0)
            product(nc.gpsimd, 0, 0)
            product(nc.vector, 0, 0)
            scalar_product(0, 0)

        for j in range(-LEAD, PAIRS + 3):
            k = j + LEAD
            new, done, moved = j - 1, j - 2, j - 3
            if k < PAIRS:
                quantise_x(k)
            if j == -1:
                start_products()
            if 0 < j < PAIRS:
                gate(j)
                new_products(j)
                scalar_product(j, 0)
            if k + 1 < PAIRS and j >= 0:
                transpose_x(k + 1)
            if 0 <= done < PAIRS:
                copy_sums(done)
            if 0 <= moved < PAIRS:
                copy_back(moved)
            if 0 <= j < PAIRS:
                for n in range(1 if j == 0 else 0, PAIR):
                    product(nc.gpsimd, j, n)
                    product(nc.vector, j, n)
            if 0 <= new < PAIRS:
                vector_sum(new)
            if k < PAIRS:
                project(k)
                add_bias(k)
                shift(k)
            if k + 2 < PAIRS and j < -1:
                transpose_x(k + 2)
            if k + LOADED < PAIRS:
                load_x((k + LOADED) * PAIR, PAIR)
            if k % 4 == 2 and k // 4 + 1 < HEIGHT // W_ROWS:
                load_w((k // 4 + 1) * W_ROWS)
            if 0 <= moved < PAIRS:
                store(moved)
            if 0 < j + 1 < PAIRS:
                weights(j + 1)
                scalar_weights(j + 1)
            if 0 <= new < PAIRS:
                tensor_sum(new)
            if 0 <= done < PAIRS:
                back(done)
            if 0 <= j < PAIRS:
                scalar_product(j, 1)
